import numpy as np
import ml_dtypes


def mxq(x, axis, fmt="e4m3"):
    dtype, down = {"e4m3": (ml_dtypes.float8_e4m3fn, 7), "e5m2": (ml_dtypes.float8_e5m2, 14)}[fmt]
    v = np.moveaxis(np.asarray(x, np.float32).astype(ml_dtypes.bfloat16).astype(np.float64), axis, -1)
    blocks = v.reshape(v.shape[:-1] + (-1, 32))
    amax = np.abs(blocks).max(-1, keepdims=True)
    byte = np.maximum(np.where(amax > 0, np.frexp(amax)[1] - 1 + 127, 0) - down, 1)
    scale = np.exp2(byte - 127.0)
    codes = (blocks / scale).astype(np.float32).astype(dtype).astype(np.float64)
    return np.moveaxis((codes * scale).reshape(v.shape), -1, axis)


WIDE = False


def mx_kscale(k):
    if not WIDE:
        return np.ones(k)
    levels = np.array([10, -10, 5, -5, 0])
    if k % 512:
        return np.exp2(np.random.permutation(np.resize(levels, k // 32))).repeat(32)
    a = np.empty((k // 512, 16))
    for p in range(k // 512):
        a[p, :8] = np.random.permutation(np.resize(levels, 8))
        for g in range(8):
            far = levels[np.abs(levels - a[p, g]) >= 10]
            a[p, g + 8] = far[np.random.randint(len(far))]
    return np.exp2(a.ravel()).repeat(32)


BF16 = ml_dtypes.bfloat16


def bf(x):
    return np.asarray(x, np.float32).astype(BF16)


def f64(x):
    return np.asarray(x).astype(np.float64)


B, I, H, AH, AI, G = 128, 128, 384, 256, 128, 4
EPS = 1e-5
K = I + H


def sigmoid(v):
    return 1.0 / (1.0 + np.exp(-v))


def ln(v, w, b):
    mu = v.mean(-1, keepdims=True)
    var = ((v - mu) ** 2).mean(-1, keepdims=True)
    return (v - mu) / np.sqrt(var + EPS) * w + b


def setup_inputs():
    n = np.random.standard_normal
    s = mx_kscale(K)
    return {
        "x": bf(n((B, I)) * s[:I]),
        "hx": bf(n((B, H)) * s[I:]),
        "ah": bf(n((B, AH))),
        "ac": bf(n((B, AH))),
        "a_w_ih": bf(n((G * AH, K)) / np.sqrt(K) / s),
        "a_w_hh": bf(n((G * AH, AH)) / np.sqrt(AH)),
        "a_ln_i_w": bf(1.0 + 0.1 * n(G * AH)),
        "a_ln_i_b": bf(0.2 * n(G * AH)),
        "a_ln_h_w": bf(1.0 + 0.1 * n(G * AH)),
        "a_ln_h_b": bf(0.2 * n(G * AH)),
        "a_ln_c_w": bf(1.0 + 0.1 * n(AH)),
        "a_ln_c_b": bf(0.2 * n(AH)),
    }


def reference(x, hx, ah, ac, a_w_ih, a_w_hh, a_ln_i_w, a_ln_i_b, a_ln_h_w, a_ln_h_b, a_ln_c_w, a_ln_c_b):
    ai = np.concatenate([f64(x), f64(hx)], axis=1)
    ig = ln(mxq(ai, 1, "e4m3") @ mxq(f64(a_w_ih), 1, "e4m3").T, f64(a_ln_i_w), f64(a_ln_i_b))
    hg = ln(f64(ah) @ f64(a_w_hh).T, f64(a_ln_h_w), f64(a_ln_h_b))
    g = ig + hg
    gi, gf, gj, go = np.split(g, G, axis=1)
    acy = ln(sigmoid(gf) * f64(ac) + sigmoid(gi) * np.tanh(gj), f64(a_ln_c_w), f64(a_ln_c_b))
    ada = sigmoid(go) * np.tanh(acy)
    return ada, acy

@@ -1,0 +1,331 @@
+from contextlib import ExitStack
+
+import concourse.mybir as mybir
+from concourse.masks import make_identity
+
+F32 = mybir.dt.float32
+BF16 = mybir.dt.bfloat16
+U32 = mybir.dt.uint32
+U8 = mybir.dt.uint8
+FP8X4 = mybir.dt.float8_e4m3fn_x4
+ALU = mybir.AluOpType
+ACT = mybir.ActivationFunctionType
+
+P = 128
+X_FEATURES = 128
+K_IH = 512
+K_HH = 256
+CELL = 256
+GATES = 4
+N = GATES * CELL
+BANK = 512
+HALVES = N // BANK
+EPS = 1e-5
+
+FLOPS = 2 * P * N * (K_IH + K_HH)
+
+
+def tile_adaptivelstmcell_pa_s_kernel(
+    tc,
+    x,
+    hx,
+    ah,
+    ac,
+    a_w_ih,
+    a_w_hh,
+    a_ln_i_w,
+    a_ln_i_b,
+    a_ln_h_w,
+    a_ln_h_b,
+    a_ln_c_w,
+    a_ln_c_b,
+    out_0,
+    out_1,
+):
+    nc = tc.nc
+    with ExitStack() as ctx:
+        keep = ctx.enter_context(tc.tile_pool(name="keep", bufs=1))
+        banks = ctx.enter_context(tc.psum_pool(name="banks", bufs=4))
+        sums = ctx.enter_context(tc.psum_pool(name="sums", bufs=1))
+
+        ident_f32 = keep.tile([P, P], F32)
+        make_identity(nc, ident_f32[:])
+        minus_half = keep.tile([P, 1], F32)
+        nc.vector.memset(minus_half[:], -0.5)
+        warm_in = keep.tile([P, 1], F32)
+        warm_out = keep.tile([P, 1], F32)
+        nc.vector.memset(warm_in[:], 0.0)
+        nc.scalar.activation(out=warm_out[:], in_=warm_in[:], func=ACT.Sigmoid)
+
+        ah_sb = keep.tile([P, K_HH], BF16)
+        nc.sync.dma_start(out=ah_sb[:], in_=ah)
+        whh_sb = keep.tile([P, GATES, 2 * K_HH], BF16)
+        whh_rows = a_w_hh.rearrange("(g p r) k -> p g (r k)", g=GATES, p=P, r=2)
+        for g in range(GATES):
+            nc.sync.dma_start(out=whh_sb[:, g, :], in_=whh_rows[:, g, :])
+
+        ln_rows = keep.tile([P, CELL], BF16)
+        nc.vector.memset(ln_rows[:], 0.0)
+        ROW_SHIFT_I, ROW_SHIFT_H, ROW_GAIN_H, LN_ROWS = 0, 4, 8, 12
+        for first_row, vector in (
+            (ROW_SHIFT_I, a_ln_i_b),
+            (ROW_SHIFT_H, a_ln_h_b),
+            (ROW_GAIN_H, a_ln_h_w),
+        ):
+            nc.sync.dma_start(
+                out=ln_rows[first_row : first_row + GATES, :],
+                in_=vector.rearrange("(r c) -> r c", c=CELL),
+            )
+
+        ai_sb = keep.tile([P, K_IH], BF16)
+        nc.sync.dma_start(out=ai_sb[:, 0:X_FEATURES], in_=x)
+        nc.sync.dma_start(out=ai_sb[:, X_FEATURES:K_IH], in_=hx)
+        wih_sb = keep.tile([P, GATES, 2 * K_IH], BF16)
+        wih_rows = a_w_ih.rearrange("(g p r) k -> p g (r k)", g=GATES, p=P, r=2)
+        for g in range(GATES):
+            nc.sync.dma_start(out=wih_sb[:, g, :], in_=wih_rows[:, g, :])
+
+        gain_i = keep.tile([P, N], BF16)
+        nc.sync.dma_start(out=gain_i[:], in_=a_ln_i_w.partition_broadcast(P))
+        ac_sb = keep.tile([P, CELL], BF16)
+        nc.sync.dma_start(out=ac_sb[:], in_=ac)
+        gain_c = keep.tile([P, CELL], BF16)
+        nc.sync.dma_start(out=gain_c[:], in_=a_ln_c_w.partition_broadcast(P))
+        shift_c = keep.tile([P, CELL], BF16)
+        nc.sync.dma_start(out=shift_c[:], in_=a_ln_c_b.partition_broadcast(P))
+
+        def spread(columns, first, name):
+            bank = banks.tile([P, 4 * P], F32, tag="bank", name=name)
+            for i in range(4):
+                nc.tensor.transpose(
+                    bank[:, i * P : (i + 1) * P],
+                    columns[:, first + i : first + i + 1].to_broadcast([P, P]),
+                    ident_f32[:],
+                )
+            return bank
+
+        def gates_in_two_banks(name):
+            two = [sums.tile([P, BANK], F32, name="%s%d" % (name, bank)) for bank in range(2)]
+            return [two[g % 2][:, (g // 2) * CELL : (g // 2 + 1) * CELL] for g in range(GATES)]
+
+        def mean_and_inverse_std(stats, count, name):
+            nc.vector.tensor_scalar_add(out=stats[:, 0, 2:3], in0=stats[:, 0, 2:3], scalar1=EPS * count)
+            mean_var = keep.tile([P, 2], F32, name=name + "_mean_var")
+            nc.vector.bn_aggr(out=mean_var[:], in_=stats[:].rearrange("p c s -> p (c s)"))
+            rstd = keep.tile([P, 1], F32, name=name + "_rstd")
+            nc.gpsimd.tensor_tensor(out=rstd[:], in0=mean_var[:, 1:2], in1=minus_half[:], op=ALU.pow)
+            return mean_var[:, 0:1], rstd[:]
+
+        ah_bank = banks.tile([P, P], F32, tag="bank")
+        nc.tensor.transpose(ah_bank[:], ah_sb[:].bitcast(F32), ident_f32[:])
+        ahT = keep.tile([P, 2, P], BF16)
+        nc.scalar.copy(
+            out=ahT[:], in_=ah_bank[:].bitcast(BF16).rearrange("p (b e) -> p e b", e=2)
+        )
+        whhT = keep.tile([P, N], F32)
+        whhT_values = whhT[:].bitcast(BF16).rearrange("p (n e) -> p n e", e=2)
+        vh = gates_in_two_banks("vh")
+        stats_h = keep.tile([P, GATES, 6], F32)
+        for g in range(GATES):
+            gate_cols = slice(g * CELL, (g + 1) * CELL)
+            whh_bank = banks.tile([P, 2, P], F32, tag="bank")
+            words = whh_sb[:, g, :].bitcast(F32)
+            for r in range(2):
+                nc.tensor.transpose(whh_bank[:, r, :], words[:, r * P : (r + 1) * P], ident_f32[:])
+            nc.scalar.copy(
+                out=whhT[:, gate_cols].rearrange("p (j r) -> p j r", r=2),
+                in_=whh_bank[:].rearrange("p r j -> p j r"),
+            )
+            for e in range(2):
+                nc.tensor.matmul(
+                    out=vh[g],
+                    lhsT=ahT[:, e, :],
+                    rhs=whhT_values[:, gate_cols, e],
+                    start=(e == 0),
+                    stop=(e == 1),
+                )
+            nc.vector.bn_stats(out=stats_h[:, g, :], in_=vh[g])
+        mean_h, rstd_h = mean_and_inverse_std(stats_h, N, "h")
+
+        ln_bank = banks.tile([P, P], F32, tag="bank")
+        nc.tensor.transpose(ln_bank[:], ln_rows[:].bitcast(F32), ident_f32[:])
+        ln_columns = keep.tile([P, LN_ROWS], F32)
+        nc.vector.tensor_copy(out=ln_columns[:], in_=ln_bank[:, 0:LN_ROWS])
+        ln_values = ln_columns[:].bitcast(BF16)
+        shift_columns = keep.tile([P, 2 * GATES], F32)
+        nc.vector.tensor_tensor(
+            out=shift_columns[:],
+            in0=ln_values[:, 2 * ROW_SHIFT_I : 2 * ROW_SHIFT_I + 2 * GATES],
+            in1=ln_values[:, 2 * ROW_SHIFT_H : 2 * ROW_SHIFT_H + 2 * GATES],
+            op=ALU.add,
+        )
+
+        ai_bank = banks.tile([P, 2, P], F32, tag="bank")
+        for u in range(2):
+            nc.tensor.transpose(
+                ai_bank[:, u, :], ai_sb[:].bitcast(F32)[:, u : 2 * P : 2], ident_f32[:]
+            )
+        ai_grouped = keep.tile([P, P, 2], F32, align_bytes=64)
+        nc.scalar.copy(out=ai_grouped[:], in_=ai_bank[:].rearrange("p u b -> p b u"))
+        ai_codes = keep.tile([P, P], U32, align_bytes=64)
+        ai_scales = keep.tile([P, P], U8, align_bytes=64)
+        nc.vector.quantize_mx(
+            out=ai_codes[:].bitcast(FP8X4),
+            scales=ai_scales[:],
+            in_=ai_grouped[:].rearrange("p b u -> p (b u)").bitcast(BF16),
+        )
+
+        w_grouped = keep.tile([P, GATES, 2 * CELL], F32, align_bytes=64)
+        w_codes = keep.tile([P, N], U32, align_bytes=64)
+        w_scales = keep.tile([P, N], U8, align_bytes=64)
+        for g in range(GATES):
+            w_bank = banks.tile([P, 4, P], F32, tag="bank")
+            words = wih_sb[:, g, :].bitcast(F32)
+            for ru in range(4):
+                first = (ru // 2) * 2 * P + ru % 2
+                nc.tensor.transpose(w_bank[:, ru, :], words[:, first : (ru // 2 + 1) * 2 * P : 2], ident_f32[:])
+            nc.scalar.copy(
+                out=w_grouped[:, g, :].rearrange("p (j r u) -> p j r u", r=2, u=2),
+                in_=w_bank[:].rearrange("p (r u) j -> p j r u", r=2, u=2),
+            )
+            gate_cols = slice(g * CELL, (g + 1) * CELL)
+            nc.vector.quantize_mx(
+                out=w_codes[:, gate_cols].bitcast(FP8X4),
+                scales=w_scales[:, gate_cols],
+                in_=w_grouped[:, g, :].bitcast(BF16),
+            )
+
+        vi = gates_in_two_banks("vi")
+        stats_i = keep.tile([P, GATES, 6], F32)
+        for g in range(GATES):
+            gate_cols = slice(g * CELL, (g + 1) * CELL)
+            nc.tensor.matmul_mx(
+                out=vi[g],
+                lhsT=ai_codes[:].bitcast(FP8X4),
+                lhsT_scale=ai_scales[:],
+                rhs=w_codes[:, gate_cols].bitcast(FP8X4),
+                rhs_scale=w_scales[:, gate_cols],
+                start=True,
+                stop=True,
+            )
+            nc.vector.bn_stats(out=stats_i[:, g, :], in_=vi[g])
+        mean_i, rstd_i = mean_and_inverse_std(stats_i, N, "i")
+
+        gain_h = keep.tile([P, BANK], F32)
+        nc.scalar.copy(out=gain_h[:], in_=spread(ln_columns, ROW_GAIN_H, "gain_h_ps")[:])
+        shift_banks = [spread(shift_columns, 4 * half, "shift_ps%d" % half) for half in range(HALVES)]
+
+        centred_h = keep.tile([P, N], F32)
+        h_part = keep.tile([P, N], F32)
+        centred_i = keep.tile([P, N], F32)
+        g_sum = keep.tile([P, N], F32)
+        gate = keep.tile([P, N], F32)
+
+        def centre_h(g):
+            cols = slice(g * CELL, (g + 1) * CELL)
+            nc.vector.scalar_tensor_tensor(
+                out=centred_h[:, cols],
+                in0=vh[g],
+                scalar=mean_h,
+                in1=gain_h[:].bitcast(BF16)[:, cols],
+                op0=ALU.subtract,
+                op1=ALU.mult,
+            )
+
+        def scale_h(g):
+            cols = slice(g * CELL, (g + 1) * CELL)
+            shift_of_gate = shift_banks[g // 2][:, (g % 2) * CELL : (g % 2 + 1) * CELL]
+            nc.vector.scalar_tensor_tensor(
+                out=h_part[:, cols].rearrange("p (w e) -> p w e", e=2),
+                in0=centred_h[:, cols].rearrange("p (w e) -> p w e", e=2),
+                scalar=rstd_h,
+                in1=shift_of_gate.rearrange("p (e w) -> p w e", e=2),
+                op0=ALU.mult,
+                op1=ALU.add,
+            )
+
+        def centre(g):
+            cols = slice(g * CELL, (g + 1) * CELL)
+            nc.vector.scalar_tensor_tensor(
+                out=centred_i[:, cols],
+                in0=vi[g],
+                scalar=mean_i,
+                in1=gain_i[:, cols],
+                op0=ALU.subtract,
+                op1=ALU.mult,
+            )
+
+        def finish(g, func):
+            cols = slice(g * CELL, (g + 1) * CELL)
+            nc.vector.scalar_tensor_tensor(
+                out=g_sum[:, cols],
+                in0=centred_i[:, cols],
+                scalar=rstd_i,
+                in1=h_part[:, cols],
+                op0=ALU.mult,
+                op1=ALU.add,
+            )
+            nc.scalar.activation(out=gate[:, cols], in_=g_sum[:, cols], func=func)
+
+        IN, FORGET, CELL_GATE, OUT = 0, 1, 2, 3
+        gate_in = gate[:, IN * CELL : (IN + 1) * CELL]
+        gate_forget = gate[:, FORGET * CELL : (FORGET + 1) * CELL]
+        gate_cell = gate[:, CELL_GATE * CELL : (CELL_GATE + 1) * CELL]
+        gate_out = gate[:, OUT * CELL : (OUT + 1) * CELL]
+
+        for g in (FORGET, IN, CELL_GATE):
+            centre_h(g)
+        for g in (FORGET, IN, CELL_GATE):
+            scale_h(g)
+        for g in (FORGET, IN, CELL_GATE):
+            centre(g)
+        finish(FORGET, ACT.Sigmoid)
+        finish(IN, ACT.Sigmoid)
+        finish(CELL_GATE, ACT.Tanh)
+
+        kept = keep.tile([P, CELL], F32)
+        nc.vector.tensor_mul(out=kept[:], in0=gate_forget, in1=ac_sb[:])
+        centre_h(OUT)
+        centre(OUT)
+        scale_h(OUT)
+        finish(OUT, ACT.Sigmoid)
+        halves = [slice(half * CELL // 2, (half + 1) * CELL // 2) for half in range(2)]
+        fresh = keep.tile([P, CELL], F32)
+        cell = keep.tile([P, CELL], F32)
+        stats_c = keep.tile([P, 2, 6], F32)
+        for cols in halves:
+            nc.vector.tensor_mul(out=fresh[:, cols], in0=gate_in[:, cols], in1=gate_cell[:, cols])
+        for cols in halves:
+            nc.vector.tensor_add(out=cell[:, cols], in0=kept[:, cols], in1=fresh[:, cols])
+        for half, cols in enumerate(halves):
+            nc.vector.bn_stats(out=stats_c[:, half, :], in_=cell[:, cols])
+        mean_c, rstd_c = mean_and_inverse_std(stats_c, CELL, "c")
+        centred_c = keep.tile([P, CELL], F32)
+        for cols in halves:
+            nc.vector.scalar_tensor_tensor(
+                out=centred_c[:, cols],
+                in0=cell[:, cols],
+                scalar=mean_c,
+                in1=gain_c[:, cols],
+                op0=ALU.subtract,
+                op1=ALU.mult,
+            )
+        acy = keep.tile([P, CELL], F32)
+        for cols in halves:
+            nc.vector.scalar_tensor_tensor(
+                out=acy[:, cols],
+                in0=centred_c[:, cols],
+                scalar=rstd_c,
+                in1=shift_c[:, cols],
+                op0=ALU.mult,
+                op1=ALU.add,
+            )
+        nc.sync.dma_start(out=out_1, in_=acy[:])
+
+        tanh_acy = keep.tile([P, CELL], F32)
+        ada = keep.tile([P, CELL], F32)
+        for cols in halves:
+            nc.scalar.activation(out=tanh_acy[:, cols], in_=acy[:, cols], func=ACT.Tanh)
+        for cols in halves:
+            nc.vector.tensor_mul(out=ada[:, cols], in0=gate_out[:, cols], in1=tanh_acy[:, cols])
+        nc.sync.dma_start(out=out_0, in_=ada[:])

@@ -19,8 +19,9 @@ CELL = 256
 GATES = 4
 N = GATES * CELL
 BANK = 512
-HALVES = N // BANK
+IN, FORGET, CELL_GATE, OUT = 0, 1, 2, 3
 EPS = 1e-5
+WARM_TRANSPOSES = 8
 
 FLOPS = 2 * P * N * (K_IH + K_HH)
 
@@ -45,48 +46,50 @@ def tile_adaptivelstmcell_pa_s_kernel(
     nc = tc.nc
     with ExitStack() as ctx:
         keep = ctx.enter_context(tc.tile_pool(name="keep", bufs=1))
-        banks = ctx.enter_context(tc.psum_pool(name="banks", bufs=4))
-        sums = ctx.enter_context(tc.psum_pool(name="sums", bufs=1))
+        banks = ctx.enter_context(tc.psum_pool(name="banks", bufs=1))
+        ctx.enter_context(tc.manual_schedule())
 
         ident_f32 = keep.tile([P, P], F32)
         make_identity(nc, ident_f32[:])
         minus_half = keep.tile([P, 1], F32)
-        nc.vector.memset(minus_half[:], -0.5)
-        warm_in = keep.tile([P, 1], F32)
+        zero = keep.tile([P, 1], F32)
         warm_out = keep.tile([P, 1], F32)
-        nc.vector.memset(warm_in[:], 0.0)
-        nc.scalar.activation(out=warm_out[:], in_=warm_in[:], func=ACT.Sigmoid)
+        nc.vector.memset(zero[:], 0.0)
+        nc.vector.memset(minus_half[:], -0.5)
+        nc.scalar.activation(out=warm_out[:], in_=zero[:], func=ACT.Sigmoid)
 
-        ah_sb = keep.tile([P, K_HH], BF16)
-        nc.sync.dma_start(out=ah_sb[:], in_=ah)
-        whh_sb = keep.tile([P, GATES, 2 * K_HH], BF16)
-        whh_rows = a_w_hh.rearrange("(g p r) k -> p g (r k)", g=GATES, p=P, r=2)
-        for g in range(GATES):
-            nc.sync.dma_start(out=whh_sb[:, g, :], in_=whh_rows[:, g, :])
-
-        ln_rows = keep.tile([P, CELL], BF16)
-        nc.vector.memset(ln_rows[:], 0.0)
-        ROW_SHIFT_I, ROW_SHIFT_H, ROW_GAIN_H, LN_ROWS = 0, 4, 8, 12
-        for first_row, vector in (
-            (ROW_SHIFT_I, a_ln_i_b),
-            (ROW_SHIFT_H, a_ln_h_b),
-            (ROW_GAIN_H, a_ln_h_w),
-        ):
-            nc.sync.dma_start(
-                out=ln_rows[first_row : first_row + GATES, :],
-                in_=vector.rearrange("(r c) -> r c", c=CELL),
-            )
+        warm_bank = banks.tile([P, BANK], F32, tag="bank7", name="warm_bank")
+        for i in range(WARM_TRANSPOSES):
+            nc.tensor.transpose(warm_bank[:, i % 4 * P : (i % 4 + 1) * P], ident_f32[:], ident_f32[:])
 
         ai_sb = keep.tile([P, K_IH], BF16)
         nc.sync.dma_start(out=ai_sb[:, 0:X_FEATURES], in_=x)
         nc.sync.dma_start(out=ai_sb[:, X_FEATURES:K_IH], in_=hx)
         wih_sb = keep.tile([P, GATES, 2 * K_IH], BF16)
+        for half in range(2):
+            nc.sync.dma_start(
+                out=wih_sb[:, 0, half * K_IH : (half + 1) * K_IH],
+                in_=a_w_ih[half * P : (half + 1) * P, :],
+            )
         wih_rows = a_w_ih.rearrange("(g p r) k -> p g (r k)", g=GATES, p=P, r=2)
-        for g in range(GATES):
+        for g in range(1, GATES):
             nc.sync.dma_start(out=wih_sb[:, g, :], in_=wih_rows[:, g, :])
-
+        ah_sb = keep.tile([P, K_HH], BF16)
+        nc.sync.dma_start(out=ah_sb[:], in_=ah)
+        whh_sb = keep.tile([P, GATES, 2 * K_HH], BF16)
+        whh_rows = a_w_hh.rearrange("(g p r) k -> p g (r k)", g=GATES, p=P, r=2)
+        for g in (0, 2):
+            nc.sync.dma_start(out=whh_sb[:, g : g + 2, :], in_=whh_rows[:, g : g + 2, :])
         gain_i = keep.tile([P, N], BF16)
         nc.sync.dma_start(out=gain_i[:], in_=a_ln_i_w.partition_broadcast(P))
+        shift_words = [keep.tile([P, GATES], F32, name="shift_words%d" % i) for i in range(2)]
+        with nc.allow_non_contiguous_dma(reason="one word a piece, 1,024 words in all"):
+            for words, vector in zip(shift_words, (a_ln_i_b, a_ln_h_b)):
+                nc.sync.dma_start(
+                    out=words[:], in_=vector.bitcast(F32).rearrange("(g w) -> w g", g=GATES)
+                )
+        gain_h = keep.tile([P, N], BF16)
+        nc.sync.dma_start(out=gain_h[:], in_=a_ln_h_w.partition_broadcast(P))
         ac_sb = keep.tile([P, CELL], BF16)
         nc.sync.dma_start(out=ac_sb[:], in_=ac)
         gain_c = keep.tile([P, CELL], BF16)
@@ -94,113 +97,112 @@ def tile_adaptivelstmcell_pa_s_kernel(
         shift_c = keep.tile([P, CELL], BF16)
         nc.sync.dma_start(out=shift_c[:], in_=a_ln_c_b.partition_broadcast(P))
 
-        def spread(columns, first, name):
-            bank = banks.tile([P, 4 * P], F32, tag="bank", name=name)
+        def bank_tile(number, name):
+            return banks.tile([P, BANK], F32, tag="bank%d" % number, name=name)
+
+        def spread(bank, columns, first):
             for i in range(4):
                 nc.tensor.transpose(
                     bank[:, i * P : (i + 1) * P],
                     columns[:, first + i : first + i + 1].to_broadcast([P, P]),
                     ident_f32[:],
                 )
-            return bank
 
-        def gates_in_two_banks(name):
-            two = [sums.tile([P, BANK], F32, name="%s%d" % (name, bank)) for bank in range(2)]
-            return [two[g % 2][:, (g // 2) * CELL : (g // 2 + 1) * CELL] for g in range(GATES)]
+        def eps_record(record, count):
+            nc.vector.memset(record[:, 0:2], 0.0)
+            nc.vector.tensor_scalar_add(out=record[:, 2:3], in0=zero[:], scalar1=EPS * count)
 
-        def mean_and_inverse_std(stats, count, name):
-            nc.vector.tensor_scalar_add(out=stats[:, 0, 2:3], in0=stats[:, 0, 2:3], scalar1=EPS * count)
+        def mean_and_inverse_std(stats, name):
             mean_var = keep.tile([P, 2], F32, name=name + "_mean_var")
-            nc.vector.bn_aggr(out=mean_var[:], in_=stats[:].rearrange("p c s -> p (c s)"))
+            nc.vector.bn_aggr(out=mean_var[:], in_=stats[:])
             rstd = keep.tile([P, 1], F32, name=name + "_rstd")
             nc.gpsimd.tensor_tensor(out=rstd[:], in0=mean_var[:, 1:2], in1=minus_half[:], op=ALU.pow)
             return mean_var[:, 0:1], rstd[:]
 
-        ah_bank = banks.tile([P, P], F32, tag="bank")
-        nc.tensor.transpose(ah_bank[:], ah_sb[:].bitcast(F32), ident_f32[:])
-        ahT = keep.tile([P, 2, P], BF16)
-        nc.scalar.copy(
-            out=ahT[:], in_=ah_bank[:].bitcast(BF16).rearrange("p (b e) -> p e b", e=2)
-        )
-        whhT = keep.tile([P, N], F32)
-        whhT_values = whhT[:].bitcast(BF16).rearrange("p (n e) -> p n e", e=2)
-        vh = gates_in_two_banks("vh")
-        stats_h = keep.tile([P, GATES, 6], F32)
-        for g in range(GATES):
-            gate_cols = slice(g * CELL, (g + 1) * CELL)
-            whh_bank = banks.tile([P, 2, P], F32, tag="bank")
-            words = whh_sb[:, g, :].bitcast(F32)
-            for r in range(2):
-                nc.tensor.transpose(whh_bank[:, r, :], words[:, r * P : (r + 1) * P], ident_f32[:])
-            nc.scalar.copy(
-                out=whhT[:, gate_cols].rearrange("p (j r) -> p j r", r=2),
-                in_=whh_bank[:].rearrange("p r j -> p j r"),
-            )
-            for e in range(2):
-                nc.tensor.matmul(
-                    out=vh[g],
-                    lhsT=ahT[:, e, :],
-                    rhs=whhT_values[:, gate_cols, e],
-                    start=(e == 0),
-                    stop=(e == 1),
-                )
-            nc.vector.bn_stats(out=stats_h[:, g, :], in_=vh[g])
-        mean_h, rstd_h = mean_and_inverse_std(stats_h, N, "h")
+        def in_bank(g):
+            return slice(g // 2 * CELL, (g // 2 + 1) * CELL)
 
-        ln_bank = banks.tile([P, P], F32, tag="bank")
-        nc.tensor.transpose(ln_bank[:], ln_rows[:].bitcast(F32), ident_f32[:])
-        ln_columns = keep.tile([P, LN_ROWS], F32)
-        nc.vector.tensor_copy(out=ln_columns[:], in_=ln_bank[:, 0:LN_ROWS])
-        ln_values = ln_columns[:].bitcast(BF16)
-        shift_columns = keep.tile([P, 2 * GATES], F32)
-        nc.vector.tensor_tensor(
-            out=shift_columns[:],
-            in0=ln_values[:, 2 * ROW_SHIFT_I : 2 * ROW_SHIFT_I + 2 * GATES],
-            in1=ln_values[:, 2 * ROW_SHIFT_H : 2 * ROW_SHIFT_H + 2 * GATES],
-            op=ALU.add,
-        )
+        SLOT = {IN: 0, CELL_GATE: 1, FORGET: 2, OUT: 3}
 
-        ai_bank = banks.tile([P, 2, P], F32, tag="bank")
-        for u in range(2):
-            nc.tensor.transpose(
-                ai_bank[:, u, :], ai_sb[:].bitcast(F32)[:, u : 2 * P : 2], ident_f32[:]
-            )
+        def of_gates(gates, vector):
+            by_pair = vector.rearrange("p (q r c) -> p r q c", q=2, r=2)[:, gates[0] % 2, :, :]
+            return by_pair[:, gates[0] // 2 : gates[-1] // 2 + 1, :]
+
+        stats_i = keep.tile([P, 6 * GATES + 3], F32)
+        eps_record(stats_i[:, 6 * GATES :], N)
+        stats_h = keep.tile([P, 3 * 7], F32)
+        nc.vector.memset(stats_h[:, 12:16:3], float(CELL))
+        eps_record(stats_h[:, 18:21], N)
+        stats_c = keep.tile([P, 3 * 5], F32)
+        eps_record(stats_c[:, 12:15], CELL)
+
         ai_grouped = keep.tile([P, P, 2], F32, align_bytes=64)
-        nc.scalar.copy(out=ai_grouped[:], in_=ai_bank[:].rearrange("p u b -> p b u"))
         ai_codes = keep.tile([P, P], U32, align_bytes=64)
         ai_scales = keep.tile([P, P], U8, align_bytes=64)
-        nc.vector.quantize_mx(
-            out=ai_codes[:].bitcast(FP8X4),
-            scales=ai_scales[:],
-            in_=ai_grouped[:].rearrange("p b u -> p (b u)").bitcast(BF16),
-        )
-
         w_grouped = keep.tile([P, GATES, 2 * CELL], F32, align_bytes=64)
         w_codes = keep.tile([P, N], U32, align_bytes=64)
         w_scales = keep.tile([P, N], U8, align_bytes=64)
-        for g in range(GATES):
-            w_bank = banks.tile([P, 4, P], F32, tag="bank")
+
+        def turn_128_rows(bank, rows, grouped):
+            for u in range(2):
+                nc.tensor.transpose(bank[:, u * P : (u + 1) * P], rows[:, u : 2 * P : 2], ident_f32[:])
+            nc.scalar.copy(
+                out=grouped.rearrange("p (b u) -> p b u", u=2),
+                in_=bank[:, 0 : 2 * P].rearrange("p (u b) -> p b u", u=2),
+            )
+
+        def turn_ai(bank_number):
+            turn_128_rows(
+                bank_tile(bank_number, "ai_bank"),
+                ai_sb[:].bitcast(F32),
+                ai_grouped[:].rearrange("p b u -> p (b u)"),
+            )
+
+        def quantise_ai():
+            nc.vector.quantize_mx(
+                out=ai_codes[:].bitcast(FP8X4),
+                scales=ai_scales[:],
+                in_=ai_grouped[:].rearrange("p b u -> p (b u)").bitcast(BF16),
+            )
+
+        def turn_half_of_first(half, bank_number):
+            turn_128_rows(
+                bank_tile(bank_number, "wih_bank0%d" % half),
+                wih_sb[:, 0, half * K_IH : (half + 1) * K_IH].bitcast(F32),
+                w_grouped[:, 0, half * CELL : (half + 1) * CELL],
+            )
+
+        def turn_wih(g, bank_number):
+            bank = bank_tile(bank_number, "wih_bank%d" % g)
             words = wih_sb[:, g, :].bitcast(F32)
             for ru in range(4):
                 first = (ru // 2) * 2 * P + ru % 2
-                nc.tensor.transpose(w_bank[:, ru, :], words[:, first : (ru // 2 + 1) * 2 * P : 2], ident_f32[:])
+                nc.tensor.transpose(
+                    bank[:, ru * P : (ru + 1) * P],
+                    words[:, first : (ru // 2 + 1) * 2 * P : 2],
+                    ident_f32[:],
+                )
             nc.scalar.copy(
                 out=w_grouped[:, g, :].rearrange("p (j r u) -> p j r u", r=2, u=2),
-                in_=w_bank[:].rearrange("p (r u) j -> p j r u", r=2, u=2),
-            )
-            gate_cols = slice(g * CELL, (g + 1) * CELL)
-            nc.vector.quantize_mx(
-                out=w_codes[:, gate_cols].bitcast(FP8X4),
-                scales=w_scales[:, gate_cols],
-                in_=w_grouped[:, g, :].bitcast(BF16),
+                in_=bank[:].rearrange("p (r u j) -> p j r u", r=2, u=2),
             )
 
-        vi = gates_in_two_banks("vi")
-        stats_i = keep.tile([P, GATES, 6], F32)
-        for g in range(GATES):
+        def quantise_columns(first, count):
+            cols = slice(first, first + count)
+            grouped = w_grouped[:].rearrange("p g c -> p (g c)")[:, 2 * first : 2 * (first + count)]
+            nc.vector.quantize_mx(
+                out=w_codes[:, cols].bitcast(FP8X4),
+                scales=w_scales[:, cols],
+                in_=grouped.bitcast(BF16),
+            )
+
+        vi = [bank_tile(4 + i, "vi%d" % i) for i in range(2)]
+        vh = [bank_tile(6 + i, "vh%d" % i) for i in range(2)]
+
+        def multiply_i(g):
             gate_cols = slice(g * CELL, (g + 1) * CELL)
             nc.tensor.matmul_mx(
-                out=vi[g],
+                out=vi[g % 2][:, in_bank(g)],
                 lhsT=ai_codes[:].bitcast(FP8X4),
                 lhsT_scale=ai_scales[:],
                 rhs=w_codes[:, gate_cols].bitcast(FP8X4),
@@ -208,98 +210,176 @@ def tile_adaptivelstmcell_pa_s_kernel(
                 start=True,
                 stop=True,
             )
-            nc.vector.bn_stats(out=stats_i[:, g, :], in_=vi[g])
-        mean_i, rstd_i = mean_and_inverse_std(stats_i, N, "i")
 
-        gain_h = keep.tile([P, BANK], F32)
-        nc.scalar.copy(out=gain_h[:], in_=spread(ln_columns, ROW_GAIN_H, "gain_h_ps")[:])
-        shift_banks = [spread(shift_columns, 4 * half, "shift_ps%d" % half) for half in range(HALVES)]
+        def stats_of_i(g):
+            nc.vector.bn_stats(out=stats_i[:, 6 * g : 6 * g + 6], in_=vi[g % 2][:, in_bank(g)])
 
-        centred_h = keep.tile([P, N], F32)
-        h_part = keep.tile([P, N], F32)
-        centred_i = keep.tile([P, N], F32)
-        g_sum = keep.tile([P, N], F32)
-        gate = keep.tile([P, N], F32)
+        ahT = keep.tile([P, 2, P], BF16)
+        whhT = keep.tile([P, N], F32)
+        whhT_values = whhT[:].bitcast(BF16).rearrange("p (n e) -> p n e", e=2)
 
-        def centre_h(g):
-            cols = slice(g * CELL, (g + 1) * CELL)
+        def turn_ah(bank_number):
+            bank = bank_tile(bank_number, "ah_bank")
+            nc.tensor.transpose(bank[:, 0:P], ah_sb[:].bitcast(F32), ident_f32[:])
+            nc.scalar.copy(
+                out=ahT[:], in_=bank[:, 0:P].bitcast(BF16).rearrange("p (b e) -> p e b", e=2)
+            )
+
+        def turn_whh(g, bank_number):
+            bank = bank_tile(bank_number, "whh_bank%d" % g)
+            words = whh_sb[:, g, :].bitcast(F32)
+            for r in range(2):
+                nc.tensor.transpose(
+                    bank[:, r * P : (r + 1) * P], words[:, r * P : (r + 1) * P], ident_f32[:]
+                )
+            nc.scalar.copy(
+                out=whhT[:, g * CELL : (g + 1) * CELL].rearrange("p (j r) -> p j r", r=2),
+                in_=bank[:, 0:CELL].rearrange("p (r j) -> p j r", r=2),
+            )
+
+        def multiply_h(g):
+            for e in range(2):
+                nc.tensor.matmul(
+                    out=vh[g % 2][:, in_bank(g)],
+                    lhsT=ahT[:, e, :],
+                    rhs=whhT_values[:, g * CELL : (g + 1) * CELL, e],
+                    start=(e == 0),
+                    stop=(e == 1),
+                )
+
+        unused = keep.tile([P, CELL], F32)
+
+        def stats_of_h_on_scalar(g, record):
+            v = vh[g % 2][:, in_bank(g)]
+            nc.scalar.activation(
+                out=unused[:], in_=v, func=ACT.Identity, scale=1.0 / CELL, accum_out=record[:, 1:2]
+            )
+            nc.scalar.activation(
+                out=unused[:],
+                in_=v,
+                func=ACT.Square,
+                scale=-1.0,
+                bias=record[:, 1:2],
+                accum_out=record[:, 2:3],
+            )
+
+        centred_i = keep.tile([P, GATES, CELL], F32)
+        i_part = keep.tile([P, GATES, CELL], F32)
+        centred_h = keep.tile([P, GATES, CELL], F32)
+        g_sum = keep.tile([P, GATES, CELL], F32)
+
+        def centre(banks_of_v, mean, gain, out, *gates):
+            bank_cols = slice(in_bank(gates[0]).start, in_bank(gates[-1]).stop)
             nc.vector.scalar_tensor_tensor(
-                out=centred_h[:, cols],
-                in0=vh[g],
-                scalar=mean_h,
-                in1=gain_h[:].bitcast(BF16)[:, cols],
+                out=out[:, SLOT[gates[0]] : SLOT[gates[-1]] + 1, :],
+                in0=banks_of_v[gates[0] % 2][:, bank_cols].rearrange("p (q c) -> p q c", c=CELL),
+                scalar=mean,
+                in1=of_gates(gates, gain[:]),
                 op0=ALU.subtract,
                 op1=ALU.mult,
             )
 
-        def scale_h(g):
-            cols = slice(g * CELL, (g + 1) * CELL)
-            shift_of_gate = shift_banks[g // 2][:, (g % 2) * CELL : (g % 2 + 1) * CELL]
+        def scale_i(*gates):
+            slots = slice(SLOT[gates[0]], SLOT[gates[-1]] + 1)
+            words = slice(gates[0] // 2 * P, (gates[-1] // 2 + 1) * P)
             nc.vector.scalar_tensor_tensor(
-                out=h_part[:, cols].rearrange("p (w e) -> p w e", e=2),
-                in0=centred_h[:, cols].rearrange("p (w e) -> p w e", e=2),
-                scalar=rstd_h,
-                in1=shift_of_gate.rearrange("p (e w) -> p w e", e=2),
-                op0=ALU.mult,
-                op1=ALU.add,
-            )
-
-        def centre(g):
-            cols = slice(g * CELL, (g + 1) * CELL)
-            nc.vector.scalar_tensor_tensor(
-                out=centred_i[:, cols],
-                in0=vi[g],
-                scalar=mean_i,
-                in1=gain_i[:, cols],
-                op0=ALU.subtract,
-                op1=ALU.mult,
-            )
-
-        def finish(g, func):
-            cols = slice(g * CELL, (g + 1) * CELL)
-            nc.vector.scalar_tensor_tensor(
-                out=g_sum[:, cols],
-                in0=centred_i[:, cols],
+                out=i_part[:, slots, :].rearrange("p q (w e) -> p (q w) e", e=2),
+                in0=centred_i[:, slots, :].rearrange("p q (w e) -> p (q w) e", e=2),
                 scalar=rstd_i,
-                in1=h_part[:, cols],
+                in1=shift_banks[gates[0] % 2][:].rearrange("p (e qw) -> p qw e", e=2)[:, words, :],
                 op0=ALU.mult,
                 op1=ALU.add,
             )
-            nc.scalar.activation(out=gate[:, cols], in_=g_sum[:, cols], func=func)
 
-        IN, FORGET, CELL_GATE, OUT = 0, 1, 2, 3
-        gate_in = gate[:, IN * CELL : (IN + 1) * CELL]
-        gate_forget = gate[:, FORGET * CELL : (FORGET + 1) * CELL]
-        gate_cell = gate[:, CELL_GATE * CELL : (CELL_GATE + 1) * CELL]
-        gate_out = gate[:, OUT * CELL : (OUT + 1) * CELL]
+        def finish(slots, cols):
+            nc.vector.scalar_tensor_tensor(
+                out=g_sum[:, slots, cols],
+                in0=centred_h[:, slots, cols],
+                scalar=rstd_h,
+                in1=i_part[:, slots, cols],
+                op0=ALU.mult,
+                op1=ALU.add,
+            )
 
-        for g in (FORGET, IN, CELL_GATE):
-            centre_h(g)
-        for g in (FORGET, IN, CELL_GATE):
-            scale_h(g)
-        for g in (FORGET, IN, CELL_GATE):
-            centre(g)
-        finish(FORGET, ACT.Sigmoid)
-        finish(IN, ACT.Sigmoid)
-        finish(CELL_GATE, ACT.Tanh)
+        turn_ai(0)
+        turn_half_of_first(0, 1)
+        turn_half_of_first(1, 2)
+        quantise_ai()
+        turn_wih(1, 3)
+        quantise_columns(0, P)
+        turn_wih(2, 0)
+        quantise_columns(P, P)
+        multiply_i(0)
+        turn_wih(3, 1)
+        quantise_columns(CELL, CELL)
+        stats_of_i(0)
+        multiply_i(1)
+        quantise_columns(2 * CELL, CELL)
+        stats_of_i(1)
+        turn_ah(2)
+        turn_whh(0, 3)
+        turn_whh(1, 0)
+        multiply_i(2)
+        quantise_columns(3 * CELL, CELL)
+        stats_of_i(2)
+        turn_whh(2, 1)
+        turn_whh(3, 2)
+        multiply_i(3)
+        stats_of_i(3)
+        shift_columns = keep.tile([P, 2 * GATES], F32)
+        nc.gpsimd.tensor_tensor(
+            out=shift_columns[:].rearrange("p (h e q) -> p q h e", h=2, e=2),
+            in0=shift_words[0][:].bitcast(BF16).rearrange("p (q h e) -> p q h e", h=2, e=2),
+            in1=shift_words[1][:].bitcast(BF16).rearrange("p (q h e) -> p q h e", h=2, e=2),
+            op=ALU.add,
+        )
+        mean_i, rstd_i = mean_and_inverse_std(stats_i, "i")
+        for g in range(GATES):
+            multiply_h(g)
+        shift_banks = [bank_tile(3, "shift0"), bank_tile(0, "shift1")]
+        for h in (1, 0):
+            spread(shift_banks[h], shift_columns, 4 * h)
+        nc.vector.bn_stats(out=stats_h[:, 0:6], in_=vh[0][:, in_bank(IN)])
+        stats_of_h_on_scalar(FORGET, stats_h[:, 12:15])
+        centre(vi, mean_i, gain_i, centred_i, FORGET)
+        nc.vector.bn_stats(out=stats_h[:, 6:12], in_=vh[0][:, in_bank(CELL_GATE)])
+        stats_of_h_on_scalar(OUT, stats_h[:, 15:18])
+        centre(vi, mean_i, gain_i, centred_i, IN, CELL_GATE)
+        scale_i(FORGET)
+        scale_i(IN, CELL_GATE)
+        mean_h, rstd_h = mean_and_inverse_std(stats_h, "h")
+        factors = keep.tile([P, 2, CELL], F32)
+        nc.scalar.copy(out=factors[:, 1, :], in_=ac_sb[:])
+        centre(vi, mean_i, gain_i, centred_i, OUT)
+        centre(vh, mean_h, gain_h, centred_h, FORGET)
+        centre(vh, mean_h, gain_h, centred_h, IN, CELL_GATE)
 
-        kept = keep.tile([P, CELL], F32)
-        nc.vector.tensor_mul(out=kept[:], in0=gate_forget, in1=ac_sb[:])
-        centre_h(OUT)
-        centre(OUT)
-        scale_h(OUT)
-        finish(OUT, ACT.Sigmoid)
         halves = [slice(half * CELL // 2, (half + 1) * CELL // 2) for half in range(2)]
-        fresh = keep.tile([P, CELL], F32)
+        in_and_forget = slice(SLOT[IN], SLOT[FORGET] + 1, SLOT[FORGET] - SLOT[IN])
+        gate_if = keep.tile([P, 2, CELL], F32)
+        gate_o = keep.tile([P, CELL], F32)
+        products = keep.tile([P, 2, CELL], F32)
         cell = keep.tile([P, CELL], F32)
-        stats_c = keep.tile([P, 2, 6], F32)
         for cols in halves:
-            nc.vector.tensor_mul(out=fresh[:, cols], in0=gate_in[:, cols], in1=gate_cell[:, cols])
+            finish(in_and_forget, cols)
+            nc.scalar.activation(
+                out=gate_if[:, :, cols], in_=g_sum[:, in_and_forget, cols], func=ACT.Sigmoid
+            )
+            finish(SLOT[CELL_GATE], cols)
+            nc.scalar.activation(
+                out=factors[:, 0, cols], in_=g_sum[:, SLOT[CELL_GATE], cols], func=ACT.Tanh
+            )
+        centre(vh, mean_h, gain_h, centred_h, OUT)
         for cols in halves:
-            nc.vector.tensor_add(out=cell[:, cols], in0=kept[:, cols], in1=fresh[:, cols])
+            nc.vector.tensor_mul(out=products[:, :, cols], in0=gate_if[:, :, cols], in1=factors[:, :, cols])
+        for cols in halves:
+            nc.vector.tensor_add(out=cell[:, cols], in0=products[:, 0, cols], in1=products[:, 1, cols])
         for half, cols in enumerate(halves):
-            nc.vector.bn_stats(out=stats_c[:, half, :], in_=cell[:, cols])
-        mean_c, rstd_c = mean_and_inverse_std(stats_c, CELL, "c")
+            nc.vector.bn_stats(out=stats_c[:, 6 * half : 6 * half + 6], in_=cell[:, cols])
+        scale_i(OUT)
+        mean_c, rstd_c = mean_and_inverse_std(stats_c, "c")
+        finish(SLOT[OUT], slice(0, CELL))
+        nc.scalar.activation(out=gate_o[:], in_=g_sum[:, SLOT[OUT], :], func=ACT.Sigmoid)
         centred_c = keep.tile([P, CELL], F32)
         for cols in halves:
             nc.vector.scalar_tensor_tensor(
@@ -327,5 +407,5 @@ def tile_adaptivelstmcell_pa_s_kernel(
         for cols in halves:
             nc.scalar.activation(out=tanh_acy[:, cols], in_=acy[:, cols], func=ACT.Tanh)
         for cols in halves:
-            nc.vector.tensor_mul(out=ada[:, cols], in0=gate_out[:, cols], in1=tanh_acy[:, cols])
+            nc.vector.tensor_mul(out=ada[:, cols], in0=gate_o[:, cols], in1=tanh_acy[:, cols])
         nc.sync.dma_start(out=out_0, in_=ada[:])

@@ -62,34 +62,36 @@ def tile_adaptivelstmcell_pa_s_kernel(
         for i in range(WARM_TRANSPOSES):
             nc.tensor.transpose(warm_bank[:, i % 4 * P : (i % 4 + 1) * P], ident_f32[:], ident_f32[:])
 
-        ai_sb = keep.tile([P, K_IH], BF16)
-        nc.sync.dma_start(out=ai_sb[:, 0:X_FEATURES], in_=x)
-        nc.sync.dma_start(out=ai_sb[:, X_FEATURES:K_IH], in_=hx)
-        wih_sb = keep.tile([P, GATES, 2 * K_IH], BF16)
-        for half in range(2):
-            nc.sync.dma_start(
-                out=wih_sb[:, 0, half * K_IH : (half + 1) * K_IH],
-                in_=a_w_ih[half * P : (half + 1) * P, :],
-            )
-        wih_rows = a_w_ih.rearrange("(g p r) k -> p g (r k)", g=GATES, p=P, r=2)
-        for g in range(1, GATES):
-            nc.sync.dma_start(out=wih_sb[:, g, :], in_=wih_rows[:, g, :])
         ah_sb = keep.tile([P, K_HH], BF16)
         nc.sync.dma_start(out=ah_sb[:], in_=ah)
         whh_sb = keep.tile([P, GATES, 2 * K_HH], BF16)
         whh_rows = a_w_hh.rearrange("(g p r) k -> p g (r k)", g=GATES, p=P, r=2)
-        for g in (0, 2):
-            nc.sync.dma_start(out=whh_sb[:, g : g + 2, :], in_=whh_rows[:, g : g + 2, :])
+        for gates in (slice(0, 1), slice(1, 2), slice(2, 4)):
+            nc.sync.dma_start(out=whh_sb[:, gates, :], in_=whh_rows[:, gates, :])
+        ai_sb = keep.tile([P, K_IH], BF16)
+        nc.sync.dma_start(out=ai_sb[:, 0:X_FEATURES], in_=x)
+        nc.sync.dma_start(out=ai_sb[:, X_FEATURES:K_IH], in_=hx)
+        wih_sb = keep.tile([P, GATES, 2 * K_IH], BF16)
+        wih_rows = a_w_ih.rearrange("(g p r) k -> p g (r k)", g=GATES, p=P, r=2)
+        gain_h_words = keep.tile([P, 4], F32)
+        shift_i_words = keep.tile([P, 4], F32)
+        shift_h_words = keep.tile([P, 4], F32)
+
+        def load_gate(g):
+            nc.sync.dma_start(out=wih_sb[:, g, :], in_=wih_rows[:, g, :])
+
+        def load_words(words, vector):
+            nc.sync.dma_start(out=words[:], in_=vector.bitcast(F32).rearrange("(w r) -> w r", r=4))
+
+        load_gate(0)
+        load_gate(1)
+        load_words(gain_h_words, a_ln_h_w)
+        load_gate(2)
+        load_words(shift_i_words, a_ln_i_b)
+        load_words(shift_h_words, a_ln_h_b)
+        load_gate(3)
         gain_i = keep.tile([P, N], BF16)
         nc.sync.dma_start(out=gain_i[:], in_=a_ln_i_w.partition_broadcast(P))
-        shift_words = [keep.tile([P, GATES], F32, name="shift_words%d" % i) for i in range(2)]
-        with nc.allow_non_contiguous_dma(reason="one word a piece, 1,024 words in all"):
-            for words, vector in zip(shift_words, (a_ln_i_b, a_ln_h_b)):
-                nc.sync.dma_start(
-                    out=words[:], in_=vector.bitcast(F32).rearrange("(g w) -> w g", g=GATES)
-                )
-        gain_h = keep.tile([P, N], BF16)
-        nc.sync.dma_start(out=gain_h[:], in_=a_ln_h_w.partition_broadcast(P))
         ac_sb = keep.tile([P, CELL], BF16)
         nc.sync.dma_start(out=ac_sb[:], in_=ac)
         gain_c = keep.tile([P, CELL], BF16)
@@ -128,11 +130,11 @@ def tile_adaptivelstmcell_pa_s_kernel(
             by_pair = vector.rearrange("p (q r c) -> p r q c", q=2, r=2)[:, gates[0] % 2, :, :]
             return by_pair[:, gates[0] // 2 : gates[-1] // 2 + 1, :]
 
-        stats_i = keep.tile([P, 6 * GATES + 3], F32)
-        eps_record(stats_i[:, 6 * GATES :], N)
-        stats_h = keep.tile([P, 3 * 7], F32)
-        nc.vector.memset(stats_h[:, 12:16:3], float(CELL))
-        eps_record(stats_h[:, 18:21], N)
+        stats_h = keep.tile([P, 6 * GATES + 3], F32)
+        eps_record(stats_h[:, 6 * GATES :], N)
+        stats_i = keep.tile([P, 3 * 7], F32)
+        nc.vector.memset(stats_i[:, 12:16:3], float(CELL))
+        eps_record(stats_i[:, 18:21], N)
         stats_c = keep.tile([P, 3 * 5], F32)
         eps_record(stats_c[:, 12:15], CELL)
 
@@ -143,19 +145,14 @@ def tile_adaptivelstmcell_pa_s_kernel(
         w_codes = keep.tile([P, N], U32, align_bytes=64)
         w_scales = keep.tile([P, N], U8, align_bytes=64)
 
-        def turn_128_rows(bank, rows, grouped):
-            for u in range(2):
-                nc.tensor.transpose(bank[:, u * P : (u + 1) * P], rows[:, u : 2 * P : 2], ident_f32[:])
-            nc.scalar.copy(
-                out=grouped.rearrange("p (b u) -> p b u", u=2),
-                in_=bank[:, 0 : 2 * P].rearrange("p (u b) -> p b u", u=2),
-            )
-
         def turn_ai(bank_number):
-            turn_128_rows(
-                bank_tile(bank_number, "ai_bank"),
-                ai_sb[:].bitcast(F32),
-                ai_grouped[:].rearrange("p b u -> p (b u)"),
+            bank = bank_tile(bank_number, "ai_bank")
+            for u in range(2):
+                nc.tensor.transpose(
+                    bank[:, u * P : (u + 1) * P], ai_sb[:].bitcast(F32)[:, u : 2 * P : 2], ident_f32[:]
+                )
+            nc.scalar.copy(
+                out=ai_grouped[:], in_=bank[:, 0 : 2 * P].rearrange("p (u b) -> p b u", u=2)
             )
 
         def quantise_ai():
@@ -163,13 +160,6 @@ def tile_adaptivelstmcell_pa_s_kernel(
                 out=ai_codes[:].bitcast(FP8X4),
                 scales=ai_scales[:],
                 in_=ai_grouped[:].rearrange("p b u -> p (b u)").bitcast(BF16),
-            )
-
-        def turn_half_of_first(half, bank_number):
-            turn_128_rows(
-                bank_tile(bank_number, "wih_bank0%d" % half),
-                wih_sb[:, 0, half * K_IH : (half + 1) * K_IH].bitcast(F32),
-                w_grouped[:, 0, half * CELL : (half + 1) * CELL],
             )
 
         def turn_wih(g, bank_number):
@@ -187,17 +177,15 @@ def tile_adaptivelstmcell_pa_s_kernel(
                 in_=bank[:].rearrange("p (r u j) -> p j r u", r=2, u=2),
             )
 
-        def quantise_columns(first, count):
-            cols = slice(first, first + count)
-            grouped = w_grouped[:].rearrange("p g c -> p (g c)")[:, 2 * first : 2 * (first + count)]
+        def quantise_wih(g):
+            gate_cols = slice(g * CELL, (g + 1) * CELL)
             nc.vector.quantize_mx(
-                out=w_codes[:, cols].bitcast(FP8X4),
-                scales=w_scales[:, cols],
-                in_=grouped.bitcast(BF16),
+                out=w_codes[:, gate_cols].bitcast(FP8X4),
+                scales=w_scales[:, gate_cols],
+                in_=w_grouped[:, g, :].bitcast(BF16),
             )
 
-        vi = [bank_tile(4 + i, "vi%d" % i) for i in range(2)]
-        vh = [bank_tile(6 + i, "vh%d" % i) for i in range(2)]
+        vh = [bank_tile(4 + i, "vh%d" % i) for i in range(2)]
 
         def multiply_i(g):
             gate_cols = slice(g * CELL, (g + 1) * CELL)
@@ -210,9 +198,6 @@ def tile_adaptivelstmcell_pa_s_kernel(
                 start=True,
                 stop=True,
             )
-
-        def stats_of_i(g):
-            nc.vector.bn_stats(out=stats_i[:, 6 * g : 6 * g + 6], in_=vi[g % 2][:, in_bank(g)])
 
         ahT = keep.tile([P, 2, P], BF16)
         whhT = keep.tile([P, N], F32)
@@ -247,10 +232,13 @@ def tile_adaptivelstmcell_pa_s_kernel(
                     stop=(e == 1),
                 )
 
+        def bn_stats(banks_of_v, stats, g):
+            nc.vector.bn_stats(out=stats[:, 6 * g : 6 * g + 6], in_=banks_of_v[g % 2][:, in_bank(g)])
+
         unused = keep.tile([P, CELL], F32)
 
-        def stats_of_h_on_scalar(g, record):
-            v = vh[g % 2][:, in_bank(g)]
+        def stats_of_i_on_scalar(g, record):
+            v = vi[g % 2][:, in_bank(g)]
             nc.scalar.activation(
                 out=unused[:], in_=v, func=ACT.Identity, scale=1.0 / CELL, accum_out=record[:, 1:2]
             )
@@ -263,8 +251,19 @@ def tile_adaptivelstmcell_pa_s_kernel(
                 accum_out=record[:, 2:3],
             )
 
+        gain_h_words_all = keep.tile([P, BANK], F32)
+        gain_h = gain_h_words_all[:].bitcast(BF16)
+
+        def spread_gain_h(bank_number):
+            bank = bank_tile(bank_number, "gain_bank")
+            spread(bank, gain_h_words, 0)
+            nc.scalar.copy(
+                out=gain_h_words_all[:].rearrange("p (w r) -> p w r", r=4),
+                in_=bank[:].rearrange("p (r w) -> p w r", r=4),
+            )
+
         centred_i = keep.tile([P, GATES, CELL], F32)
-        i_part = keep.tile([P, GATES, CELL], F32)
+        h_part = keep.tile([P, GATES, CELL], F32)
         centred_h = keep.tile([P, GATES, CELL], F32)
         g_sum = keep.tile([P, GATES, CELL], F32)
 
@@ -274,85 +273,91 @@ def tile_adaptivelstmcell_pa_s_kernel(
                 out=out[:, SLOT[gates[0]] : SLOT[gates[-1]] + 1, :],
                 in0=banks_of_v[gates[0] % 2][:, bank_cols].rearrange("p (q c) -> p q c", c=CELL),
                 scalar=mean,
-                in1=of_gates(gates, gain[:]),
+                in1=of_gates(gates, gain),
                 op0=ALU.subtract,
                 op1=ALU.mult,
             )
 
-        def scale_i(*gates):
-            slots = slice(SLOT[gates[0]], SLOT[gates[-1]] + 1)
-            words = slice(gates[0] // 2 * P, (gates[-1] // 2 + 1) * P)
-            nc.vector.scalar_tensor_tensor(
-                out=i_part[:, slots, :].rearrange("p q (w e) -> p (q w) e", e=2),
-                in0=centred_i[:, slots, :].rearrange("p q (w e) -> p (q w) e", e=2),
-                scalar=rstd_i,
-                in1=shift_banks[gates[0] % 2][:].rearrange("p (e qw) -> p qw e", e=2)[:, words, :],
-                op0=ALU.mult,
-                op1=ALU.add,
-            )
+        def scale_h(g):
+            octets = [t[:, SLOT[g], :].rearrange("p (w c) -> p w c", c=8) for t in (h_part, centred_h)]
+            words = slice(32 * g, 32 * g + 32)
+            for half in range(2):
+                quads = slice(4 * half, 4 * half + 4)
+                nc.vector.scalar_tensor_tensor(
+                    out=octets[0][:, :, quads],
+                    in0=octets[1][:, :, quads],
+                    scalar=rstd_h,
+                    in1=shift_banks[half][:].rearrange("p (c w) -> p w c", c=4)[:, words, :],
+                    op0=ALU.mult,
+                    op1=ALU.add,
+                )
 
         def finish(slots, cols):
             nc.vector.scalar_tensor_tensor(
                 out=g_sum[:, slots, cols],
-                in0=centred_h[:, slots, cols],
-                scalar=rstd_h,
-                in1=i_part[:, slots, cols],
+                in0=centred_i[:, slots, cols],
+                scalar=rstd_i,
+                in1=h_part[:, slots, cols],
                 op0=ALU.mult,
                 op1=ALU.add,
             )
 
-        turn_ai(0)
-        turn_half_of_first(0, 1)
-        turn_half_of_first(1, 2)
-        quantise_ai()
-        turn_wih(1, 3)
-        quantise_columns(0, P)
-        turn_wih(2, 0)
-        quantise_columns(P, P)
-        multiply_i(0)
-        turn_wih(3, 1)
-        quantise_columns(CELL, CELL)
-        stats_of_i(0)
-        multiply_i(1)
-        quantise_columns(2 * CELL, CELL)
-        stats_of_i(1)
         turn_ah(2)
-        turn_whh(0, 3)
-        turn_whh(1, 0)
-        multiply_i(2)
-        quantise_columns(3 * CELL, CELL)
-        stats_of_i(2)
-        turn_whh(2, 1)
+        turn_whh(0, 0)
+        turn_whh(1, 1)
+        turn_whh(2, 3)
         turn_whh(3, 2)
-        multiply_i(3)
-        stats_of_i(3)
-        shift_columns = keep.tile([P, 2 * GATES], F32)
+        multiply_h(0)
+        bn_stats(vh, stats_h, 0)
+        multiply_h(1)
+        bn_stats(vh, stats_h, 1)
+        turn_ai(6)
+        turn_wih(0, 0)
+        multiply_h(2)
+        bn_stats(vh, stats_h, 2)
+        multiply_h(3)
+        bn_stats(vh, stats_h, 3)
+        mean_h, rstd_h = mean_and_inverse_std(stats_h, "h")
+        quantise_ai()
+        turn_wih(1, 1)
+        quantise_wih(0)
+        turn_wih(2, 3)
+        quantise_wih(1)
+        spread_gain_h(0)
+        turn_wih(3, 2)
+        vi = [bank_tile(6 + i, "vi%d" % i) for i in range(2)]
+        multiply_i(0)
+        bn_stats(vi, stats_i, 0)
+        quantise_wih(2)
+        multiply_i(1)
+        bn_stats(vi, stats_i, 1)
+        centre(vh, mean_h, gain_h, centred_h, FORGET)
+        quantise_wih(3)
+        shift_columns = keep.tile([P, 8], F32)
         nc.gpsimd.tensor_tensor(
-            out=shift_columns[:].rearrange("p (h e q) -> p q h e", h=2, e=2),
-            in0=shift_words[0][:].bitcast(BF16).rearrange("p (q h e) -> p q h e", h=2, e=2),
-            in1=shift_words[1][:].bitcast(BF16).rearrange("p (q h e) -> p q h e", h=2, e=2),
+            out=shift_columns[:],
+            in0=shift_i_words[:].bitcast(BF16),
+            in1=shift_h_words[:].bitcast(BF16),
             op=ALU.add,
         )
+        shift_banks = [bank_tile(1, "shift0"), bank_tile(3, "shift1")]
+        for half in range(2):
+            spread(shift_banks[half], shift_columns, 4 * half)
+        multiply_i(2)
+        stats_of_i_on_scalar(2, stats_i[:, 12:15])
+        multiply_i(3)
+        stats_of_i_on_scalar(3, stats_i[:, 15:18])
+        centre(vh, mean_h, gain_h, centred_h, IN, CELL_GATE)
+        scale_h(FORGET)
+        scale_h(IN)
+        scale_h(CELL_GATE)
         mean_i, rstd_i = mean_and_inverse_std(stats_i, "i")
-        for g in range(GATES):
-            multiply_h(g)
-        shift_banks = [bank_tile(3, "shift0"), bank_tile(0, "shift1")]
-        for h in (1, 0):
-            spread(shift_banks[h], shift_columns, 4 * h)
-        nc.vector.bn_stats(out=stats_h[:, 0:6], in_=vh[0][:, in_bank(IN)])
-        stats_of_h_on_scalar(FORGET, stats_h[:, 12:15])
-        centre(vi, mean_i, gain_i, centred_i, FORGET)
-        nc.vector.bn_stats(out=stats_h[:, 6:12], in_=vh[0][:, in_bank(CELL_GATE)])
-        stats_of_h_on_scalar(OUT, stats_h[:, 15:18])
-        centre(vi, mean_i, gain_i, centred_i, IN, CELL_GATE)
-        scale_i(FORGET)
-        scale_i(IN, CELL_GATE)
-        mean_h, rstd_h = mean_and_inverse_std(stats_h, "h")
+        centre(vh, mean_h, gain_h, centred_h, OUT)
+        centre(vi, mean_i, gain_i[:], centred_i, FORGET)
+        centre(vi, mean_i, gain_i[:], centred_i, IN, CELL_GATE)
+        centre(vi, mean_i, gain_i[:], centred_i, OUT)
         factors = keep.tile([P, 2, CELL], F32)
         nc.scalar.copy(out=factors[:, 1, :], in_=ac_sb[:])
-        centre(vi, mean_i, gain_i, centred_i, OUT)
-        centre(vh, mean_h, gain_h, centred_h, FORGET)
-        centre(vh, mean_h, gain_h, centred_h, IN, CELL_GATE)
 
         halves = [slice(half * CELL // 2, (half + 1) * CELL // 2) for half in range(2)]
         in_and_forget = slice(SLOT[IN], SLOT[FORGET] + 1, SLOT[FORGET] - SLOT[IN])
@@ -369,17 +374,16 @@ def tile_adaptivelstmcell_pa_s_kernel(
             nc.scalar.activation(
                 out=factors[:, 0, cols], in_=g_sum[:, SLOT[CELL_GATE], cols], func=ACT.Tanh
             )
-        centre(vh, mean_h, gain_h, centred_h, OUT)
+        scale_h(OUT)
         for cols in halves:
             nc.vector.tensor_mul(out=products[:, :, cols], in0=gate_if[:, :, cols], in1=factors[:, :, cols])
         for cols in halves:
             nc.vector.tensor_add(out=cell[:, cols], in0=products[:, 0, cols], in1=products[:, 1, cols])
         for half, cols in enumerate(halves):
             nc.vector.bn_stats(out=stats_c[:, 6 * half : 6 * half + 6], in_=cell[:, cols])
-        scale_i(OUT)
-        mean_c, rstd_c = mean_and_inverse_std(stats_c, "c")
         finish(SLOT[OUT], slice(0, CELL))
         nc.scalar.activation(out=gate_o[:], in_=g_sum[:, SLOT[OUT], :], func=ACT.Sigmoid)
+        mean_c, rstd_c = mean_and_inverse_std(stats_c, "c")
         centred_c = keep.tile([P, CELL], F32)
         for cols in halves:
             nc.vector.scalar_tensor_tensor(

@@ -21,7 +21,6 @@ N = GATES * CELL
 BANK = 512
 IN, FORGET, CELL_GATE, OUT = 0, 1, 2, 3
 EPS = 1e-5
-WARM_TRANSPOSES = 8
 
 FLOPS = 2 * P * N * (K_IH + K_HH)
 
@@ -57,10 +56,6 @@ def tile_adaptivelstmcell_pa_s_kernel(
         nc.vector.memset(zero[:], 0.0)
         nc.vector.memset(minus_half[:], -0.5)
         nc.scalar.activation(out=warm_out[:], in_=zero[:], func=ACT.Sigmoid)
-
-        warm_bank = banks.tile([P, BANK], F32, tag="bank7", name="warm_bank")
-        for i in range(WARM_TRANSPOSES):
-            nc.tensor.transpose(warm_bank[:, i % 4 * P : (i % 4 + 1) * P], ident_f32[:], ident_f32[:])
 
         ah_sb = keep.tile([P, K_HH], BF16)
         nc.sync.dma_start(out=ah_sb[:], in_=ah)
@@ -292,15 +287,16 @@ def tile_adaptivelstmcell_pa_s_kernel(
                     op1=ALU.add,
                 )
 
-        def finish(slots, cols):
+        def finish(g, func, gate):
             nc.vector.scalar_tensor_tensor(
-                out=g_sum[:, slots, cols],
-                in0=centred_i[:, slots, cols],
+                out=g_sum[:, SLOT[g], :],
+                in0=centred_i[:, SLOT[g], :],
                 scalar=rstd_i,
-                in1=h_part[:, slots, cols],
+                in1=h_part[:, SLOT[g], :],
                 op0=ALU.mult,
                 op1=ALU.add,
             )
+            nc.scalar.activation(out=gate[:], in_=g_sum[:, SLOT[g], :], func=func)
 
         turn_ah(2)
         turn_whh(0, 0)
@@ -356,33 +352,27 @@ def tile_adaptivelstmcell_pa_s_kernel(
         centre(vi, mean_i, gain_i[:], centred_i, FORGET)
         centre(vi, mean_i, gain_i[:], centred_i, IN, CELL_GATE)
         centre(vi, mean_i, gain_i[:], centred_i, OUT)
-        factors = keep.tile([P, 2, CELL], F32)
-        nc.scalar.copy(out=factors[:, 1, :], in_=ac_sb[:])
 
+        gate_in = keep.tile([P, CELL], F32)
+        gate_forget = keep.tile([P, CELL], F32)
+        gate_cell = keep.tile([P, CELL], F32)
+        gate_out = keep.tile([P, CELL], F32)
+        finish(FORGET, ACT.Sigmoid, gate_forget)
+        finish(IN, ACT.Sigmoid, gate_in)
+        finish(CELL_GATE, ACT.Tanh, gate_cell)
+        kept = keep.tile([P, CELL], F32)
+        nc.vector.tensor_mul(out=kept[:], in0=gate_forget[:], in1=ac_sb[:])
+        scale_h(OUT)
         halves = [slice(half * CELL // 2, (half + 1) * CELL // 2) for half in range(2)]
-        in_and_forget = slice(SLOT[IN], SLOT[FORGET] + 1, SLOT[FORGET] - SLOT[IN])
-        gate_if = keep.tile([P, 2, CELL], F32)
-        gate_o = keep.tile([P, CELL], F32)
-        products = keep.tile([P, 2, CELL], F32)
+        fresh = keep.tile([P, CELL], F32)
         cell = keep.tile([P, CELL], F32)
         for cols in halves:
-            finish(in_and_forget, cols)
-            nc.scalar.activation(
-                out=gate_if[:, :, cols], in_=g_sum[:, in_and_forget, cols], func=ACT.Sigmoid
-            )
-            finish(SLOT[CELL_GATE], cols)
-            nc.scalar.activation(
-                out=factors[:, 0, cols], in_=g_sum[:, SLOT[CELL_GATE], cols], func=ACT.Tanh
-            )
-        scale_h(OUT)
+            nc.vector.tensor_mul(out=fresh[:, cols], in0=gate_in[:, cols], in1=gate_cell[:, cols])
         for cols in halves:
-            nc.vector.tensor_mul(out=products[:, :, cols], in0=gate_if[:, :, cols], in1=factors[:, :, cols])
-        for cols in halves:
-            nc.vector.tensor_add(out=cell[:, cols], in0=products[:, 0, cols], in1=products[:, 1, cols])
+            nc.vector.tensor_add(out=cell[:, cols], in0=kept[:, cols], in1=fresh[:, cols])
         for half, cols in enumerate(halves):
             nc.vector.bn_stats(out=stats_c[:, 6 * half : 6 * half + 6], in_=cell[:, cols])
-        finish(SLOT[OUT], slice(0, CELL))
-        nc.scalar.activation(out=gate_o[:], in_=g_sum[:, SLOT[OUT], :], func=ACT.Sigmoid)
+        finish(OUT, ACT.Sigmoid, gate_out)
         mean_c, rstd_c = mean_and_inverse_std(stats_c, "c")
         centred_c = keep.tile([P, CELL], F32)
         for cols in halves:
@@ -411,5 +401,5 @@ def tile_adaptivelstmcell_pa_s_kernel(
         for cols in halves:
             nc.scalar.activation(out=tanh_acy[:, cols], in_=acy[:, cols], func=ACT.Tanh)
         for cols in halves:
-            nc.vector.tensor_mul(out=ada[:, cols], in0=gate_o[:, cols], in1=tanh_acy[:, cols])
+            nc.vector.tensor_mul(out=ada[:, cols], in0=gate_out[:, cols], in1=tanh_acy[:, cols])
         nc.sync.dma_start(out=out_0, in_=ada[:])

@@ -21,6 +21,7 @@ N = GATES * CELL
 BANK = 512
 IN, FORGET, CELL_GATE, OUT = 0, 1, 2, 3
 EPS = 1e-5
+WARM_COLUMNS = 340
 
 FLOPS = 2 * P * N * (K_IH + K_HH)
 
@@ -48,6 +49,8 @@ def tile_adaptivelstmcell_pa_s_kernel(
         banks = ctx.enter_context(tc.psum_pool(name="banks", bufs=1))
         ctx.enter_context(tc.manual_schedule())
 
+        zeros = keep.tile([P, WARM_COLUMNS], F32)
+        nc.vector.memset(zeros[:], 0.0)
         ident_f32 = keep.tile([P, P], F32)
         make_identity(nc, ident_f32[:])
         minus_half = keep.tile([P, 1], F32)
@@ -56,6 +59,11 @@ def tile_adaptivelstmcell_pa_s_kernel(
         nc.vector.memset(zero[:], 0.0)
         nc.vector.memset(minus_half[:], -0.5)
         nc.scalar.activation(out=warm_out[:], in_=zero[:], func=ACT.Sigmoid)
+
+        warm_bank = banks.tile([P, BANK], F32, tag="bank7", name="warm_bank")
+        nc.tensor.matmul(
+            out=warm_bank[:, 0:WARM_COLUMNS], lhsT=zeros[:, 0:P], rhs=zeros[:], start=True, stop=True
+        )
 
         ah_sb = keep.tile([P, K_HH], BF16)
         nc.sync.dma_start(out=ah_sb[:], in_=ah)
@@ -68,22 +76,24 @@ def tile_adaptivelstmcell_pa_s_kernel(
         nc.sync.dma_start(out=ai_sb[:, X_FEATURES:K_IH], in_=hx)
         wih_sb = keep.tile([P, GATES, 2 * K_IH], BF16)
         wih_rows = a_w_ih.rearrange("(g p r) k -> p g (r k)", g=GATES, p=P, r=2)
-        gain_h_words = keep.tile([P, 4], F32)
-        shift_i_words = keep.tile([P, 4], F32)
-        shift_h_words = keep.tile([P, 4], F32)
+        ln_rows = keep.tile([P, CELL], BF16)
+        nc.vector.memset(ln_rows[:], 0.0)
+        ROW_GAIN_H, ROW_SHIFT_I, ROW_SHIFT_H, LN_ROWS = 0, 4, 8, 12
 
         def load_gate(g):
             nc.sync.dma_start(out=wih_sb[:, g, :], in_=wih_rows[:, g, :])
 
-        def load_words(words, vector):
-            nc.sync.dma_start(out=words[:], in_=vector.bitcast(F32).rearrange("(w r) -> w r", r=4))
+        def load_rows(first, vector):
+            nc.sync.dma_start(
+                out=ln_rows[first : first + GATES, :], in_=vector.rearrange("(r c) -> r c", c=CELL)
+            )
 
         load_gate(0)
+        load_rows(ROW_GAIN_H, a_ln_h_w)
+        load_rows(ROW_SHIFT_I, a_ln_i_b)
         load_gate(1)
-        load_words(gain_h_words, a_ln_h_w)
+        load_rows(ROW_SHIFT_H, a_ln_h_b)
         load_gate(2)
-        load_words(shift_i_words, a_ln_i_b)
-        load_words(shift_h_words, a_ln_h_b)
         load_gate(3)
         gain_i = keep.tile([P, N], BF16)
         nc.sync.dma_start(out=gain_i[:], in_=a_ln_i_w.partition_broadcast(P))
@@ -127,9 +137,9 @@ def tile_adaptivelstmcell_pa_s_kernel(
 
         stats_h = keep.tile([P, 6 * GATES + 3], F32)
         eps_record(stats_h[:, 6 * GATES :], N)
-        stats_i = keep.tile([P, 3 * 7], F32)
-        nc.vector.memset(stats_i[:, 12:16:3], float(CELL))
-        eps_record(stats_i[:, 18:21], N)
+        stats_i = keep.tile([P, 3 * 8], F32)
+        nc.vector.memset(stats_i[:, 18:19], float(CELL))
+        eps_record(stats_i[:, 21:24], N)
         stats_c = keep.tile([P, 3 * 5], F32)
         eps_record(stats_c[:, 12:15], CELL)
 
@@ -246,16 +256,29 @@ def tile_adaptivelstmcell_pa_s_kernel(
                 accum_out=record[:, 2:3],
             )
 
-        gain_h_words_all = keep.tile([P, BANK], F32)
-        gain_h = gain_h_words_all[:].bitcast(BF16)
+        ln_columns = keep.tile([P, LN_ROWS], F32)
+        gain_h_words = keep.tile([P, BANK], F32)
+        gain_h = gain_h_words[:].bitcast(BF16)
+        shift_columns = keep.tile([P, 2 * GATES], F32)
+
+        def turn_ln_rows(bank_number):
+            bank = bank_tile(bank_number, "ln_bank")
+            nc.tensor.transpose(bank[:, 0:P], ln_rows[:].bitcast(F32), ident_f32[:])
+            nc.scalar.copy(out=ln_columns[:], in_=bank[:, 0:LN_ROWS])
+
+        def add_shifts():
+            values = ln_columns[:].bitcast(BF16)
+            rows_i, rows_h = [
+                values[:, 2 * first : 2 * (first + GATES)].rearrange("p (q h e) -> p q h e", h=2, e=2)
+                for first in (ROW_SHIFT_I, ROW_SHIFT_H)
+            ]
+            out = shift_columns[:].rearrange("p (h e q) -> p q h e", h=2, e=2)
+            nc.gpsimd.tensor_tensor(out=out, in0=rows_i, in1=rows_h, op=ALU.add)
 
         def spread_gain_h(bank_number):
             bank = bank_tile(bank_number, "gain_bank")
-            spread(bank, gain_h_words, 0)
-            nc.scalar.copy(
-                out=gain_h_words_all[:].rearrange("p (w r) -> p w r", r=4),
-                in_=bank[:].rearrange("p (r w) -> p w r", r=4),
-            )
+            spread(bank, ln_columns, ROW_GAIN_H)
+            nc.scalar.copy(out=gain_h_words[:], in_=bank[:])
 
         centred_i = keep.tile([P, GATES, CELL], F32)
         h_part = keep.tile([P, GATES, CELL], F32)
@@ -273,19 +296,17 @@ def tile_adaptivelstmcell_pa_s_kernel(
                 op1=ALU.mult,
             )
 
-        def scale_h(g):
-            octets = [t[:, SLOT[g], :].rearrange("p (w c) -> p w c", c=8) for t in (h_part, centred_h)]
-            words = slice(32 * g, 32 * g + 32)
-            for half in range(2):
-                quads = slice(4 * half, 4 * half + 4)
-                nc.vector.scalar_tensor_tensor(
-                    out=octets[0][:, :, quads],
-                    in0=octets[1][:, :, quads],
-                    scalar=rstd_h,
-                    in1=shift_banks[half][:].rearrange("p (c w) -> p w c", c=4)[:, words, :],
-                    op0=ALU.mult,
-                    op1=ALU.add,
-                )
+        def scale_h(*gates):
+            slots = slice(SLOT[gates[0]], SLOT[gates[-1]] + 1)
+            words = slice(gates[0] // 2 * P, (gates[-1] // 2 + 1) * P)
+            nc.vector.scalar_tensor_tensor(
+                out=h_part[:, slots, :].rearrange("p q (w e) -> p (q w) e", e=2),
+                in0=centred_h[:, slots, :].rearrange("p q (w e) -> p (q w) e", e=2),
+                scalar=rstd_h,
+                in1=shift_banks[gates[0] % 2][:].rearrange("p (e qw) -> p qw e", e=2)[:, words, :],
+                op0=ALU.mult,
+                op1=ALU.add,
+            )
 
         def finish(g, func, gate):
             nc.vector.scalar_tensor_tensor(
@@ -315,40 +336,33 @@ def tile_adaptivelstmcell_pa_s_kernel(
         bn_stats(vh, stats_h, 3)
         mean_h, rstd_h = mean_and_inverse_std(stats_h, "h")
         quantise_ai()
+        turn_ln_rows(7)
+        add_shifts()
         turn_wih(1, 1)
         quantise_wih(0)
         turn_wih(2, 3)
         quantise_wih(1)
-        spread_gain_h(0)
         turn_wih(3, 2)
+        spread_gain_h(0)
         vi = [bank_tile(6 + i, "vi%d" % i) for i in range(2)]
         multiply_i(0)
         bn_stats(vi, stats_i, 0)
         quantise_wih(2)
         multiply_i(1)
         bn_stats(vi, stats_i, 1)
-        centre(vh, mean_h, gain_h, centred_h, FORGET)
         quantise_wih(3)
-        shift_columns = keep.tile([P, 8], F32)
-        nc.gpsimd.tensor_tensor(
-            out=shift_columns[:],
-            in0=shift_i_words[:].bitcast(BF16),
-            in1=shift_h_words[:].bitcast(BF16),
-            op=ALU.add,
-        )
         shift_banks = [bank_tile(1, "shift0"), bank_tile(3, "shift1")]
-        for half in range(2):
-            spread(shift_banks[half], shift_columns, 4 * half)
+        for h in range(2):
+            spread(shift_banks[h], shift_columns, 4 * h)
         multiply_i(2)
-        stats_of_i_on_scalar(2, stats_i[:, 12:15])
+        bn_stats(vi, stats_i, 2)
         multiply_i(3)
-        stats_of_i_on_scalar(3, stats_i[:, 15:18])
+        stats_of_i_on_scalar(3, stats_i[:, 18:21])
+        centre(vh, mean_h, gain_h, centred_h, FORGET, OUT)
         centre(vh, mean_h, gain_h, centred_h, IN, CELL_GATE)
-        scale_h(FORGET)
-        scale_h(IN)
-        scale_h(CELL_GATE)
+        scale_h(FORGET, OUT)
+        scale_h(IN, CELL_GATE)
         mean_i, rstd_i = mean_and_inverse_std(stats_i, "i")
-        centre(vh, mean_h, gain_h, centred_h, OUT)
         centre(vi, mean_i, gain_i[:], centred_i, FORGET)
         centre(vi, mean_i, gain_i[:], centred_i, IN, CELL_GATE)
         centre(vi, mean_i, gain_i[:], centred_i, OUT)
@@ -362,7 +376,6 @@ def tile_adaptivelstmcell_pa_s_kernel(
         finish(CELL_GATE, ACT.Tanh, gate_cell)
         kept = keep.tile([P, CELL], F32)
         nc.vector.tensor_mul(out=kept[:], in0=gate_forget[:], in1=ac_sb[:])
-        scale_h(OUT)
         halves = [slice(half * CELL // 2, (half + 1) * CELL // 2) for half in range(2)]
         fresh = keep.tile([P, CELL], F32)
         cell = keep.tile([P, CELL], F32)

@@ -351,21 +351,20 @@ def tile_adaptivelstmcell_pa_s_kernel(
         multiply_i(1)
         bn_stats(vi, stats_i, 1)
         quantise_wih(3)
-        shift_banks = [bank_tile(1, "shift0"), bank_tile(3, "shift1")]
-        for h in range(2):
-            spread(shift_banks[h], shift_columns, 4 * h)
         multiply_i(2)
         bn_stats(vi, stats_i, 2)
         multiply_i(3)
         stats_of_i_on_scalar(3, stats_i[:, 18:21])
+        shift_banks = [bank_tile(1, "shift0"), bank_tile(3, "shift1")]
+        for h in (1, 0):
+            spread(shift_banks[h], shift_columns, 4 * h)
         centre(vh, mean_h, gain_h, centred_h, FORGET, OUT)
         centre(vh, mean_h, gain_h, centred_h, IN, CELL_GATE)
-        scale_h(FORGET, OUT)
-        scale_h(IN, CELL_GATE)
         mean_i, rstd_i = mean_and_inverse_std(stats_i, "i")
+        scale_h(FORGET)
+        scale_h(IN, CELL_GATE)
         centre(vi, mean_i, gain_i[:], centred_i, FORGET)
         centre(vi, mean_i, gain_i[:], centred_i, IN, CELL_GATE)
-        centre(vi, mean_i, gain_i[:], centred_i, OUT)
 
         gate_in = keep.tile([P, CELL], F32)
         gate_forget = keep.tile([P, CELL], F32)
@@ -376,6 +375,7 @@ def tile_adaptivelstmcell_pa_s_kernel(
         finish(CELL_GATE, ACT.Tanh, gate_cell)
         kept = keep.tile([P, CELL], F32)
         nc.vector.tensor_mul(out=kept[:], in0=gate_forget[:], in1=ac_sb[:])
+        centre(vi, mean_i, gain_i[:], centred_i, OUT)
         halves = [slice(half * CELL // 2, (half + 1) * CELL // 2) for half in range(2)]
         fresh = keep.tile([P, CELL], F32)
         cell = keep.tile([P, CELL], F32)
@@ -385,7 +385,7 @@ def tile_adaptivelstmcell_pa_s_kernel(
             nc.vector.tensor_add(out=cell[:, cols], in0=kept[:, cols], in1=fresh[:, cols])
         for half, cols in enumerate(halves):
             nc.vector.bn_stats(out=stats_c[:, 6 * half : 6 * half + 6], in_=cell[:, cols])
-        finish(OUT, ACT.Sigmoid, gate_out)
+        scale_h(OUT)
         mean_c, rstd_c = mean_and_inverse_std(stats_c, "c")
         centred_c = keep.tile([P, CELL], F32)
         for cols in halves:
@@ -397,6 +397,7 @@ def tile_adaptivelstmcell_pa_s_kernel(
                 op0=ALU.subtract,
                 op1=ALU.mult,
             )
+        finish(OUT, ACT.Sigmoid, gate_out)
         acy = keep.tile([P, CELL], F32)
         for cols in halves:
             nc.vector.scalar_tensor_tensor(

@@ -89,11 +89,11 @@ def tile_adaptivelstmcell_pa_s_kernel(
             )
 
         load_gate(0)
-        load_rows(ROW_GAIN_H, a_ln_h_w)
-        load_rows(ROW_SHIFT_I, a_ln_i_b)
         load_gate(1)
-        load_rows(ROW_SHIFT_H, a_ln_h_b)
+        load_rows(ROW_GAIN_H, a_ln_h_w)
         load_gate(2)
+        load_rows(ROW_SHIFT_I, a_ln_i_b)
+        load_rows(ROW_SHIFT_H, a_ln_h_b)
         load_gate(3)
         gain_i = keep.tile([P, N], BF16)
         nc.sync.dma_start(out=gain_i[:], in_=a_ln_i_w.partition_broadcast(P))
@@ -336,14 +336,13 @@ def tile_adaptivelstmcell_pa_s_kernel(
         bn_stats(vh, stats_h, 3)
         mean_h, rstd_h = mean_and_inverse_std(stats_h, "h")
         quantise_ai()
-        turn_ln_rows(7)
-        add_shifts()
         turn_wih(1, 1)
         quantise_wih(0)
         turn_wih(2, 3)
         quantise_wih(1)
+        turn_ln_rows(7)
+        add_shifts()
         turn_wih(3, 2)
-        spread_gain_h(0)
         vi = [bank_tile(6 + i, "vi%d" % i) for i in range(2)]
         multiply_i(0)
         bn_stats(vi, stats_i, 0)
@@ -351,13 +350,14 @@ def tile_adaptivelstmcell_pa_s_kernel(
         multiply_i(1)
         bn_stats(vi, stats_i, 1)
         quantise_wih(3)
+        spread_gain_h(0)
+        shift_banks = [bank_tile(1, "shift0"), bank_tile(3, "shift1")]
+        for h in range(2):
+            spread(shift_banks[h], shift_columns, 4 * h)
         multiply_i(2)
         bn_stats(vi, stats_i, 2)
         multiply_i(3)
         stats_of_i_on_scalar(3, stats_i[:, 18:21])
-        shift_banks = [bank_tile(1, "shift0"), bank_tile(3, "shift1")]
-        for h in (1, 0):
-            spread(shift_banks[h], shift_columns, 4 * h)
         centre(vh, mean_h, gain_h, centred_h, FORGET, OUT)
         centre(vh, mean_h, gain_h, centred_h, IN, CELL_GATE)
         mean_i, rstd_i = mean_and_inverse_std(stats_i, "i")

from contextlib import ExitStack

import concourse.mybir as mybir
from concourse.masks import make_identity

F32 = mybir.dt.float32
BF16 = mybir.dt.bfloat16
U32 = mybir.dt.uint32
U8 = mybir.dt.uint8
FP8X4 = mybir.dt.float8_e4m3fn_x4
ALU = mybir.AluOpType
ACT = mybir.ActivationFunctionType

P = 128
X_FEATURES = 128
K_IH = 512
K_HH = 256
CELL = 256
GATES = 4
N = GATES * CELL
BANK = 512
IN, FORGET, CELL_GATE, OUT = 0, 1, 2, 3
EPS = 1e-5
WARM_COLUMNS = 340

FLOPS = 2 * P * N * (K_IH + K_HH)


def tile_adaptivelstmcell_pa_s_kernel(
    tc,
    x,
    hx,
    ah,
    ac,
    a_w_ih,
    a_w_hh,
    a_ln_i_w,
    a_ln_i_b,
    a_ln_h_w,
    a_ln_h_b,
    a_ln_c_w,
    a_ln_c_b,
    out_0,
    out_1,
):
    nc = tc.nc
    with ExitStack() as ctx:
        keep = ctx.enter_context(tc.tile_pool(name="keep", bufs=1))
        banks = ctx.enter_context(tc.psum_pool(name="banks", bufs=1))
        ctx.enter_context(tc.manual_schedule())

        zeros = keep.tile([P, WARM_COLUMNS], F32)
        nc.vector.memset(zeros[:], 0.0)
        ident_f32 = keep.tile([P, P], F32)
        make_identity(nc, ident_f32[:])
        minus_half = keep.tile([P, 1], F32)
        zero = keep.tile([P, 1], F32)
        warm_out = keep.tile([P, 1], F32)
        nc.vector.memset(zero[:], 0.0)
        nc.vector.memset(minus_half[:], -0.5)
        nc.scalar.activation(out=warm_out[:], in_=zero[:], func=ACT.Sigmoid)

        warm_bank = banks.tile([P, BANK], F32, tag="bank7", name="warm_bank")
        nc.tensor.matmul(
            out=warm_bank[:, 0:WARM_COLUMNS], lhsT=zeros[:, 0:P], rhs=zeros[:], start=True, stop=True
        )

        ah_sb = keep.tile([P, K_HH], BF16)
        nc.sync.dma_start(out=ah_sb[:], in_=ah)
        whh_sb = keep.tile([P, GATES, 2 * K_HH], BF16)
        whh_rows = a_w_hh.rearrange("(g p r) k -> p g (r k)", g=GATES, p=P, r=2)
        for gates in (slice(0, 1), slice(1, 2), slice(2, 4)):
            nc.sync.dma_start(out=whh_sb[:, gates, :], in_=whh_rows[:, gates, :])
        ai_sb = keep.tile([P, K_IH], BF16)
        nc.sync.dma_start(out=ai_sb[:, 0:X_FEATURES], in_=x)
        nc.sync.dma_start(out=ai_sb[:, X_FEATURES:K_IH], in_=hx)
        wih_sb = keep.tile([P, GATES, 2 * K_IH], BF16)
        wih_rows = a_w_ih.rearrange("(g p r) k -> p g (r k)", g=GATES, p=P, r=2)
        ln_rows = keep.tile([P, CELL], BF16)
        nc.vector.memset(ln_rows[:], 0.0)
        ROW_GAIN_H, ROW_SHIFT_I, ROW_SHIFT_H, LN_ROWS = 0, 4, 8, 12

        def load_gate(g):
            nc.sync.dma_start(out=wih_sb[:, g, :], in_=wih_rows[:, g, :])

        def load_rows(first, vector):
            nc.sync.dma_start(
                out=ln_rows[first : first + GATES, :], in_=vector.rearrange("(r c) -> r c", c=CELL)
            )

        load_gate(0)
        load_gate(1)
        load_rows(ROW_GAIN_H, a_ln_h_w)
        load_gate(2)
        load_rows(ROW_SHIFT_I, a_ln_i_b)
        load_rows(ROW_SHIFT_H, a_ln_h_b)
        load_gate(3)
        gain_i = keep.tile([P, N], BF16)
        nc.sync.dma_start(out=gain_i[:], in_=a_ln_i_w.partition_broadcast(P))
        ac_sb = keep.tile([P, CELL], BF16)
        nc.sync.dma_start(out=ac_sb[:], in_=ac)
        gain_c = keep.tile([P, CELL], BF16)
        nc.sync.dma_start(out=gain_c[:], in_=a_ln_c_w.partition_broadcast(P))
        shift_c = keep.tile([P, CELL], BF16)
        nc.sync.dma_start(out=shift_c[:], in_=a_ln_c_b.partition_broadcast(P))

        def bank_tile(number, name):
            return banks.tile([P, BANK], F32, tag="bank%d" % number, name=name)

        def spread(bank, columns, first):
            for i in range(4):
                nc.tensor.transpose(
                    bank[:, i * P : (i + 1) * P],
                    columns[:, first + i : first + i + 1].to_broadcast([P, P]),
                    ident_f32[:],
                )

        def eps_record(record, count):
            nc.vector.memset(record[:, 0:2], 0.0)
            nc.vector.tensor_scalar_add(out=record[:, 2:3], in0=zero[:], scalar1=EPS * count)

        def mean_and_inverse_std(stats, name):
            mean_var = keep.tile([P, 2], F32, name=name + "_mean_var")
            nc.vector.bn_aggr(out=mean_var[:], in_=stats[:])
            rstd = keep.tile([P, 1], F32, name=name + "_rstd")
            nc.gpsimd.tensor_tensor(out=rstd[:], in0=mean_var[:, 1:2], in1=minus_half[:], op=ALU.pow)
            return mean_var[:, 0:1], rstd[:]

        def in_bank(g):
            return slice(g // 2 * CELL, (g // 2 + 1) * CELL)

        SLOT = {IN: 0, CELL_GATE: 1, FORGET: 2, OUT: 3}

        def of_gates(gates, vector):
            by_pair = vector.rearrange("p (q r c) -> p r q c", q=2, r=2)[:, gates[0] % 2, :, :]
            return by_pair[:, gates[0] // 2 : gates[-1] // 2 + 1, :]

        stats_h = keep.tile([P, 6 * GATES + 3], F32)
        eps_record(stats_h[:, 6 * GATES :], N)
        stats_i = keep.tile([P, 3 * 8], F32)
        nc.vector.memset(stats_i[:, 18:19], float(CELL))
        eps_record(stats_i[:, 21:24], N)
        stats_c = keep.tile([P, 3 * 5], F32)
        eps_record(stats_c[:, 12:15], CELL)

        ai_grouped = keep.tile([P, P, 2], F32, align_bytes=64)
        ai_codes = keep.tile([P, P], U32, align_bytes=64)
        ai_scales = keep.tile([P, P], U8, align_bytes=64)
        w_grouped = keep.tile([P, GATES, 2 * CELL], F32, align_bytes=64)
        w_codes = keep.tile([P, N], U32, align_bytes=64)
        w_scales = keep.tile([P, N], U8, align_bytes=64)

        def turn_ai(bank_number):
            bank = bank_tile(bank_number, "ai_bank")
            for u in range(2):
                nc.tensor.transpose(
                    bank[:, u * P : (u + 1) * P], ai_sb[:].bitcast(F32)[:, u : 2 * P : 2], ident_f32[:]
                )
            nc.scalar.copy(
                out=ai_grouped[:], in_=bank[:, 0 : 2 * P].rearrange("p (u b) -> p b u", u=2)
            )

        def quantise_ai():
            nc.vector.quantize_mx(
                out=ai_codes[:].bitcast(FP8X4),
                scales=ai_scales[:],
                in_=ai_grouped[:].rearrange("p b u -> p (b u)").bitcast(BF16),
            )

        def turn_wih(g, bank_number):
            bank = bank_tile(bank_number, "wih_bank%d" % g)
            words = wih_sb[:, g, :].bitcast(F32)
            for ru in range(4):
                first = (ru // 2) * 2 * P + ru % 2
                nc.tensor.transpose(
                    bank[:, ru * P : (ru + 1) * P],
                    words[:, first : (ru // 2 + 1) * 2 * P : 2],
                    ident_f32[:],
                )
            nc.scalar.copy(
                out=w_grouped[:, g, :].rearrange("p (j r u) -> p j r u", r=2, u=2),
                in_=bank[:].rearrange("p (r u j) -> p j r u", r=2, u=2),
            )

        def quantise_wih(g):
            gate_cols = slice(g * CELL, (g + 1) * CELL)
            nc.vector.quantize_mx(
                out=w_codes[:, gate_cols].bitcast(FP8X4),
                scales=w_scales[:, gate_cols],
                in_=w_grouped[:, g, :].bitcast(BF16),
            )

        vh = [bank_tile(4 + i, "vh%d" % i) for i in range(2)]

        def multiply_i(g):
            gate_cols = slice(g * CELL, (g + 1) * CELL)
            nc.tensor.matmul_mx(
                out=vi[g % 2][:, in_bank(g)],
                lhsT=ai_codes[:].bitcast(FP8X4),
                lhsT_scale=ai_scales[:],
                rhs=w_codes[:, gate_cols].bitcast(FP8X4),
                rhs_scale=w_scales[:, gate_cols],
                start=True,
                stop=True,
            )

        ahT = keep.tile([P, 2, P], BF16)
        whhT = keep.tile([P, N], F32)
        whhT_values = whhT[:].bitcast(BF16).rearrange("p (n e) -> p n e", e=2)

        def turn_ah(bank_number):
            bank = bank_tile(bank_number, "ah_bank")
            nc.tensor.transpose(bank[:, 0:P], ah_sb[:].bitcast(F32), ident_f32[:])
            nc.scalar.copy(
                out=ahT[:], in_=bank[:, 0:P].bitcast(BF16).rearrange("p (b e) -> p e b", e=2)
            )

        def turn_whh(g, bank_number):
            bank = bank_tile(bank_number, "whh_bank%d" % g)
            words = whh_sb[:, g, :].bitcast(F32)
            for r in range(2):
                nc.tensor.transpose(
                    bank[:, r * P : (r + 1) * P], words[:, r * P : (r + 1) * P], ident_f32[:]
                )
            nc.scalar.copy(
                out=whhT[:, g * CELL : (g + 1) * CELL].rearrange("p (j r) -> p j r", r=2),
                in_=bank[:, 0:CELL].rearrange("p (r j) -> p j r", r=2),
            )

        def multiply_h(g):
            for e in range(2):
                nc.tensor.matmul(
                    out=vh[g % 2][:, in_bank(g)],
                    lhsT=ahT[:, e, :],
                    rhs=whhT_values[:, g * CELL : (g + 1) * CELL, e],
                    start=(e == 0),
                    stop=(e == 1),
                )

        def bn_stats(banks_of_v, stats, g):
            nc.vector.bn_stats(out=stats[:, 6 * g : 6 * g + 6], in_=banks_of_v[g % 2][:, in_bank(g)])

        unused = keep.tile([P, CELL], F32)

        def stats_of_i_on_scalar(g, record):
            v = vi[g % 2][:, in_bank(g)]
            nc.scalar.activation(
                out=unused[:], in_=v, func=ACT.Identity, scale=1.0 / CELL, accum_out=record[:, 1:2]
            )
            nc.scalar.activation(
                out=unused[:],
                in_=v,
                func=ACT.Square,
                scale=-1.0,
                bias=record[:, 1:2],
                accum_out=record[:, 2:3],
            )

        ln_columns = keep.tile([P, LN_ROWS], F32)
        gain_h_words = keep.tile([P, BANK], F32)
        gain_h = gain_h_words[:].bitcast(BF16)
        shift_columns = keep.tile([P, 2 * GATES], F32)

        def turn_ln_rows(bank_number):
            bank = bank_tile(bank_number, "ln_bank")
            nc.tensor.transpose(bank[:, 0:P], ln_rows[:].bitcast(F32), ident_f32[:])
            nc.scalar.copy(out=ln_columns[:], in_=bank[:, 0:LN_ROWS])

        def add_shifts():
            values = ln_columns[:].bitcast(BF16)
            rows_i, rows_h = [
                values[:, 2 * first : 2 * (first + GATES)].rearrange("p (q h e) -> p q h e", h=2, e=2)
                for first in (ROW_SHIFT_I, ROW_SHIFT_H)
            ]
            out = shift_columns[:].rearrange("p (h e q) -> p q h e", h=2, e=2)
            nc.gpsimd.tensor_tensor(out=out, in0=rows_i, in1=rows_h, op=ALU.add)

        def spread_gain_h(bank_number):
            bank = bank_tile(bank_number, "gain_bank")
            spread(bank, ln_columns, ROW_GAIN_H)
            nc.scalar.copy(out=gain_h_words[:], in_=bank[:])

        centred_i = keep.tile([P, GATES, CELL], F32)
        h_part = keep.tile([P, GATES, CELL], F32)
        centred_h = keep.tile([P, GATES, CELL], F32)
        g_sum = keep.tile([P, GATES, CELL], F32)

        def centre(banks_of_v, mean, gain, out, *gates):
            bank_cols = slice(in_bank(gates[0]).start, in_bank(gates[-1]).stop)
            nc.vector.scalar_tensor_tensor(
                out=out[:, SLOT[gates[0]] : SLOT[gates[-1]] + 1, :],
                in0=banks_of_v[gates[0] % 2][:, bank_cols].rearrange("p (q c) -> p q c", c=CELL),
                scalar=mean,
                in1=of_gates(gates, gain),
                op0=ALU.subtract,
                op1=ALU.mult,
            )

        def scale_h(*gates):
            slots = slice(SLOT[gates[0]], SLOT[gates[-1]] + 1)
            words = slice(gates[0] // 2 * P, (gates[-1] // 2 + 1) * P)
            nc.vector.scalar_tensor_tensor(
                out=h_part[:, slots, :].rearrange("p q (w e) -> p (q w) e", e=2),
                in0=centred_h[:, slots, :].rearrange("p q (w e) -> p (q w) e", e=2),
                scalar=rstd_h,
                in1=shift_banks[gates[0] % 2][:].rearrange("p (e qw) -> p qw e", e=2)[:, words, :],
                op0=ALU.mult,
                op1=ALU.add,
            )

        def finish(g, func, gate):
            nc.vector.scalar_tensor_tensor(
                out=g_sum[:, SLOT[g], :],
                in0=centred_i[:, SLOT[g], :],
                scalar=rstd_i,
                in1=h_part[:, SLOT[g], :],
                op0=ALU.mult,
                op1=ALU.add,
            )
            nc.scalar.activation(out=gate[:], in_=g_sum[:, SLOT[g], :], func=func)

        turn_ah(2)
        turn_whh(0, 0)
        turn_whh(1, 1)
        turn_whh(2, 3)
        turn_whh(3, 2)
        multiply_h(0)
        bn_stats(vh, stats_h, 0)
        multiply_h(1)
        bn_stats(vh, stats_h, 1)
        turn_ai(6)
        turn_wih(0, 0)
        multiply_h(2)
        bn_stats(vh, stats_h, 2)
        multiply_h(3)
        bn_stats(vh, stats_h, 3)
        mean_h, rstd_h = mean_and_inverse_std(stats_h, "h")
        quantise_ai()
        turn_wih(1, 1)
        quantise_wih(0)
        turn_wih(2, 3)
        quantise_wih(1)
        turn_ln_rows(7)
        add_shifts()
        turn_wih(3, 2)
        vi = [bank_tile(6 + i, "vi%d" % i) for i in range(2)]
        multiply_i(0)
        bn_stats(vi, stats_i, 0)
        quantise_wih(2)
        multiply_i(1)
        bn_stats(vi, stats_i, 1)
        quantise_wih(3)
        spread_gain_h(0)
        shift_banks = [bank_tile(1, "shift0"), bank_tile(3, "shift1")]
        for h in range(2):
            spread(shift_banks[h], shift_columns, 4 * h)
        multiply_i(2)
        bn_stats(vi, stats_i, 2)
        multiply_i(3)
        stats_of_i_on_scalar(3, stats_i[:, 18:21])
        centre(vh, mean_h, gain_h, centred_h, FORGET, OUT)
        centre(vh, mean_h, gain_h, centred_h, IN, CELL_GATE)
        mean_i, rstd_i = mean_and_inverse_std(stats_i, "i")
        scale_h(FORGET)
        scale_h(IN, CELL_GATE)
        centre(vi, mean_i, gain_i[:], centred_i, FORGET)
        centre(vi, mean_i, gain_i[:], centred_i, IN, CELL_GATE)

        gate_in = keep.tile([P, CELL], F32)
        gate_forget = keep.tile([P, CELL], F32)
        gate_cell = keep.tile([P, CELL], F32)
        gate_out = keep.tile([P, CELL], F32)
        finish(FORGET, ACT.Sigmoid, gate_forget)
        finish(IN, ACT.Sigmoid, gate_in)
        finish(CELL_GATE, ACT.Tanh, gate_cell)
        kept = keep.tile([P, CELL], F32)
        nc.vector.tensor_mul(out=kept[:], in0=gate_forget[:], in1=ac_sb[:])
        centre(vi, mean_i, gain_i[:], centred_i, OUT)
        halves = [slice(half * CELL // 2, (half + 1) * CELL // 2) for half in range(2)]
        fresh = keep.tile([P, CELL], F32)
        cell = keep.tile([P, CELL], F32)
        for cols in halves:
            nc.vector.tensor_mul(out=fresh[:, cols], in0=gate_in[:, cols], in1=gate_cell[:, cols])
        for cols in halves:
            nc.vector.tensor_add(out=cell[:, cols], in0=kept[:, cols], in1=fresh[:, cols])
        for half, cols in enumerate(halves):
            nc.vector.bn_stats(out=stats_c[:, 6 * half : 6 * half + 6], in_=cell[:, cols])
        scale_h(OUT)
        mean_c, rstd_c = mean_and_inverse_std(stats_c, "c")
        centred_c = keep.tile([P, CELL], F32)
        for cols in halves:
            nc.vector.scalar_tensor_tensor(
                out=centred_c[:, cols],
                in0=cell[:, cols],
                scalar=mean_c,
                in1=gain_c[:, cols],
                op0=ALU.subtract,
                op1=ALU.mult,
            )
        finish(OUT, ACT.Sigmoid, gate_out)
        acy = keep.tile([P, CELL], F32)
        for cols in halves:
            nc.vector.scalar_tensor_tensor(
                out=acy[:, cols],
                in0=centred_c[:, cols],
                scalar=rstd_c,
                in1=shift_c[:, cols],
                op0=ALU.mult,
                op1=ALU.add,
            )
        nc.sync.dma_start(out=out_1, in_=acy[:])

        tanh_acy = keep.tile([P, CELL], F32)
        ada = keep.tile([P, CELL], F32)
        for cols in halves:
            nc.scalar.activation(out=tanh_acy[:, cols], in_=acy[:, cols], func=ACT.Tanh)
        for cols in halves:
            nc.vector.tensor_mul(out=ada[:, cols], in0=gate_out[:, cols], in1=tanh_acy[:, cols])
        nc.sync.dma_start(out=out_0, in_=ada[:])
